import numpy as np
import ml_dtypes


def mxq(x, axis, fmt="e4m3"):
    dtype, down = {"e4m3": (ml_dtypes.float8_e4m3fn, 7), "e5m2": (ml_dtypes.float8_e5m2, 14)}[fmt]
    v = np.moveaxis(np.asarray(x, np.float32).astype(ml_dtypes.bfloat16).astype(np.float64), axis, -1)
    blocks = v.reshape(v.shape[:-1] + (-1, 32))
    amax = np.abs(blocks).max(-1, keepdims=True)
    byte = np.maximum(np.where(amax > 0, np.frexp(amax)[1] - 1 + 127, 0) - down, 1)
    scale = np.exp2(byte - 127.0)
    codes = (blocks / scale).astype(np.float32).astype(dtype).astype(np.float64)
    return np.moveaxis((codes * scale).reshape(v.shape), -1, axis)


WIDE = False


def mx_kscale(k):
    if not WIDE:
        return np.ones(k)
    levels = np.array([10, -10, 5, -5, 0])
    a = np.random.permutation(np.resize(levels, k // 512 * 4)).reshape(k // 512, 4)
    idx = np.arange(k)
    return np.exp2(a[idx // 512, idx % 128 // 32])


BF16 = ml_dtypes.bfloat16


def bf(x):
    return np.asarray(x, np.float32).astype(BF16)


def f64(x):
    return np.asarray(x).astype(np.float64)


B, S, D = 512, 16, 512
EPS = 1e-9


def layernorm(x, gain, bias_):
    mu = x.mean(-1, keepdims=True)
    sd = x.std(-1, keepdims=True)
    return gain * (x - mu) / (sd + EPS) + bias_


def setup_inputs():
    s, t = mx_kscale(D), mx_kscale(D)
    return {
        "c_att": bf(np.random.standard_normal((B, S, D)) * 0.4 * s),
        "mlp_kernel_1": bf(np.random.standard_normal((D, D)) / np.sqrt(D) / s[:, None]),
        "mlp_kernel_2": bf(np.random.standard_normal((D, D)) / np.sqrt(D) / t[:, None]),
        "mlp_gain_1": bf((1.0 + 0.1 * np.random.standard_normal(D)) * t),
        "mlp_gain_2": bf(1.0 + 0.1 * np.random.standard_normal(D)),
        "mlp_bias_1": bf(0.1 * np.random.standard_normal(D) * t),
        "mlp_bias_2": bf(0.1 * np.random.standard_normal(D)),
    }


def reference(c_att, mlp_kernel_1, mlp_kernel_2, mlp_gain_1, mlp_gain_2, mlp_bias_1, mlp_bias_2):
    y1 = mxq(f64(c_att), 2, "e4m3") @ mxq(f64(mlp_kernel_1), 0, "e4m3")
    h = np.maximum(layernorm(y1, f64(mlp_gain_1), f64(mlp_bias_1)), 0.0)
    y2 = mxq(h, 2, "e4m3") @ mxq(f64(mlp_kernel_2), 0, "e4m3")
    return layernorm(y2, f64(mlp_gain_2), f64(mlp_bias_2))

@@ -1,0 +1,336 @@
+from contextlib import ExitStack
+
+import concourse.mybir as mybir
+from concourse.masks import make_identity
+
+F32 = mybir.dt.float32
+BF16 = mybir.dt.bfloat16
+U32 = mybir.dt.uint32
+U8 = mybir.dt.uint8
+FP8X4 = mybir.dt.float8_e4m3fn_x4
+ACT = mybir.ActivationFunctionType
+ALU = mybir.AluOpType
+
+P = 128
+D = 512
+TOKENS = 512 * 16
+PAIR = 2 * P
+NPAIR = TOKENS // PAIR
+EPS = 1e-9
+FLOPS = 2 * 2 * TOKENS * D * D
+LOAD_AHEAD = 6
+MANUAL = True
+
+
+def tile_rlstmcell_pa_t_kernel(tc, c_att, w1, w2, g1, g2, b1, b2, out):
+    nc = tc.nc
+    x_pairs = c_att.flatten_outer_dims().rearrange("(q p i) d -> q p (i d)", p=P, i=2)
+    o_pairs = out.flatten_outer_dims().rearrange("(q p i) d -> q p (i d)", p=P, i=2)
+
+    with ExitStack() as ctx:
+        if MANUAL:
+            ctx.enter_context(tc.manual_schedule())
+        const = ctx.enter_context(tc.tile_pool(name="const", bufs=1))
+        xin = ctx.enter_context(tc.tile_pool(name="xin", bufs=LOAD_AHEAD + 3))
+        work = ctx.enter_context(tc.tile_pool(name="work", bufs=2))
+        tail = ctx.enter_context(tc.tile_pool(name="tail", bufs=3))
+        small = ctx.enter_context(tc.tile_pool(name="small", bufs=3))
+        ps_xt = ctx.enter_context(tc.psum_pool(name="ps_xt", bufs=1))
+        ps_y1 = ctx.enter_context(tc.psum_pool(name="ps_y1", bufs=2))
+        ps_zt = ctx.enter_context(tc.psum_pool(name="ps_zt", bufs=2))
+        ps_y2 = ctx.enter_context(tc.psum_pool(name="ps_y2", bufs=3))
+
+        x_t = {}
+        xt_t = {}
+        xg_t = {}
+        xq_t = {}
+        y1_t = {}
+        z_t = {}
+        zt_t = {}
+        ht_t = {}
+        hg_t = {}
+        hq_t = {}
+        y2_t = {}
+        a_t = {}
+        st_t = {}
+
+        def valid(q):
+            return 0 <= q < NPAIR
+
+        def load_x(q):
+            if not valid(q):
+                return
+            x_sb = xin.tile([P, 2 * D], BF16, name="x_sb")
+            nc.sync.dma_start(out=x_sb[:], in_=x_pairs[q])
+            x_t[q] = x_sb
+
+        for q in range(2):
+            load_x(q)
+        gbr = const.tile([P, P], BF16, name="gbr")
+        nc.vector.memset(gbr[:], 0.0)
+        nc.scalar.dma_start(out=gbr[0:4, :], in_=g1.rearrange("(j p) -> j p", p=P))
+        nc.scalar.dma_start(out=gbr[4:8, :], in_=b1.rearrange("(j p) -> j p", p=P))
+        w1raw = const.tile([P, 4, D], BF16, name="w1raw")
+        nc.scalar.dma_start(
+            out=w1raw[:].rearrange("p (u e) n -> p u (e n)", u=2),
+            in_=w1.rearrange("(u p e) n -> p u (e n)", u=2, e=2),
+        )
+        w2raw = const.tile([P, 4, D], BF16, name="w2raw")
+        nc.scalar.dma_start(out=w2raw[:], in_=w2.rearrange("(t p) n -> p t n", p=P))
+        g2b = const.tile([P, D], BF16, name="g2b")
+        nc.scalar.dma_start(out=g2b[:], in_=g2.partition_broadcast(P))
+        b2b = const.tile([P, D], BF16, name="b2b")
+        nc.scalar.dma_start(out=b2b[:], in_=b2.partition_broadcast(P))
+        for q in range(2, LOAD_AHEAD):
+            load_x(q)
+
+        one = const.tile([P, 1], F32, name="one")
+        nc.vector.memset(one[:], 1.0)
+        nc.scalar.activation(out=one[:], in_=one[:], func=ACT.Sqrt)
+
+        ident = const.tile([P, P], F32, name="ident")
+        make_identity(nc, ident[:])
+
+        gbf = const.tile([P, P], F32, name="gbf")
+        nc.vector.tensor_copy(out=gbf[:], in_=gbr[:])
+        gbt = ps_zt.tile([P, 2, PAIR], F32, name="zt")
+        nc.tensor.transpose(gbt[:, 0, 0:P], gbf[:], ident[:])
+        gb1 = const.tile([P, 8], F32, name="gb1")
+        nc.vector.tensor_copy(out=gb1[:], in_=gbt[:, 0, 0:8])
+
+        w1g = const.tile([P, D, 4], BF16, name="w1g", align_bytes=64)
+        w1q = const.tile([P, D], U32, name="w1q", align_bytes=64)
+        w1s = const.tile([P, D], U8, name="w1s", align_bytes=64)
+        w2g = const.tile([P, D, 4], BF16, name="w2g", align_bytes=64)
+        w2q = const.tile([P, D], U32, name="w2q", align_bytes=64)
+        w2s = const.tile([P, D], U8, name="w2s", align_bytes=64)
+        g2f = const.tile([P, D], F32, name="g2f")
+        b2f = const.tile([P, D], F32, name="b2f")
+        nc.vector.tensor_copy(out=w1g[:], in_=w1raw[:].rearrange("p t n -> p n t"))
+        nc.vector.quantize_mx(
+            out=w1q[:].bitcast(FP8X4), scales=w1s[:], in_=w1g[:].rearrange("p n t -> p (n t)")
+        )
+
+        def v_prepare_late(step):
+            if step == 0:
+                nc.vector.tensor_copy(out=w2g[:], in_=w2raw[:].rearrange("p t n -> p n t"))
+            else:
+                nc.vector.quantize_mx(
+                    out=w2q[:].bitcast(FP8X4), scales=w2s[:],
+                    in_=w2g[:].rearrange("p n t -> p (n t)"),
+                )
+                nc.vector.tensor_copy(out=g2f[:], in_=g2b[:])
+                nc.vector.tensor_copy(out=b2f[:], in_=b2b[:])
+
+        def pe_xt(q):
+            if not valid(q):
+                return
+            xt = ps_xt.tile([P, 2, 2, P], F32, name="xt")
+            x32 = x_t[q][:].bitcast(F32)
+            for i in range(2):
+                for u in range(2):
+                    c0 = 256 * i + 128 * u
+                    nc.tensor.transpose(xt[:, i, u, :], x32[:, c0 : c0 + P], ident[:])
+            xt_t[q] = xt
+
+        def s_xevac(q):
+            if not valid(q):
+                return
+            xg = work.tile([P, 4 * PAIR], BF16, name="xg", align_bytes=64)
+            nc.scalar.copy(
+                out=xg[:].bitcast(F32).rearrange("p (i w u) -> p i w u", i=2, u=2),
+                in_=xt_t[q][:].rearrange("p i u w -> p i w u"),
+            )
+            xg_t[q] = xg
+
+        def v_quant_x(q):
+            if not valid(q):
+                return
+            xq = work.tile([P, PAIR], U32, name="xq", align_bytes=64)
+            xs = work.tile([P, PAIR], U8, name="xs", align_bytes=64)
+            nc.vector.quantize_mx(out=xq[:].bitcast(FP8X4), scales=xs[:], in_=xg_t[q][:])
+            xq_t[q] = (xq, xs)
+
+        def pe_mx(q, src, wq, ws, pool, nm, dst):
+            if not valid(q):
+                return
+            codes, scales = src[q]
+            banks = []
+            for i in range(2):
+                acc = pool.tile([P, D], F32, name=nm)
+                cols = slice(i * P, (i + 1) * P)
+                nc.tensor.matmul_mx(
+                    out=acc[:],
+                    lhsT=codes[:, cols].bitcast(FP8X4),
+                    lhsT_scale=scales[:, cols],
+                    rhs=wq[:].bitcast(FP8X4),
+                    rhs_scale=ws[:],
+                    start=True,
+                    stop=True,
+                )
+                banks.append(acc)
+            dst[q] = banks
+
+        def span(t):
+            lo = 0 if valid(t) else 2
+            hi = 4 if valid(t - 2) else 2
+            return lo, hi
+
+        def new_stats(t):
+            lo, hi = span(t)
+            if lo >= hi:
+                return
+            st = small.tile([P, 4, 6], F32, name="st")
+            mv = small.tile([P, 4, 2], F32, name="mv")
+            sd = small.tile([P, 4], F32, name="sd")
+            rr = small.tile([P, 4], F32, name="rr")
+            nmr = None
+            if valid(t):
+                nmr = small.tile([P, 2], F32, name="nmr")
+            st_t[t] = (st, mv, sd, rr, nmr)
+
+        def v_stats(t, q, banks, base):
+            if not valid(q):
+                return
+            st, mv = st_t[t][0], st_t[t][1]
+            for i in range(2):
+                nc.vector.bn_stats(out=st[:, base + i, :], in_=banks[q][i][:])
+            for i in range(2):
+                nc.vector.bn_aggr(out=mv[:, base + i, :], in_=st[:, base + i, :])
+
+        def s_sqrt(t):
+            lo, hi = span(t)
+            if lo >= hi:
+                return
+            mv, sd = st_t[t][1], st_t[t][2]
+            nc.scalar.activation(out=sd[:, lo:hi], in_=mv[:, lo:hi, 1], func=ACT.Sqrt)
+
+        def v_small(t):
+            lo, hi = span(t)
+            if lo >= hi:
+                return
+            st, mv, sd, rr, nmr = st_t[t]
+            nc.vector.tensor_scalar_add(out=sd[:, lo:hi], in0=sd[:, lo:hi], scalar1=EPS)
+            nc.vector.reciprocal(out=rr[:, lo:hi], in_=sd[:, lo:hi])
+            if valid(t):
+                nc.vector.scalar_tensor_tensor(
+                    out=nmr[:], in0=mv[:, 0:2, 0], scalar=-1.0, in1=rr[:, 0:2],
+                    op0=ALU.mult, op1=ALU.mult,
+                )
+
+        def s_z1(q):
+            if not valid(q):
+                return
+            rr, nmr = st_t[q][3], st_t[q][4]
+            z = work.tile([P, 2, D], F32, name="z")
+            for i in range(2):
+                nc.scalar.activation(
+                    out=z[:, i, :], in_=y1_t[q][i][:], func=ACT.Identity,
+                    scale=rr[:, i : i + 1], bias=nmr[:, i : i + 1],
+                )
+            z_t[q] = z
+
+        def pe_zt(q):
+            if not valid(q):
+                return
+            z = z_t[q]
+            banks = []
+            for h in range(2):
+                zt = ps_zt.tile([P, 2, PAIR], F32, name="zt")
+                banks.append(zt)
+            for i in range(2):
+                for j in range(4):
+                    nc.tensor.transpose(
+                        banks[j // 2][:, j % 2, i * P : (i + 1) * P],
+                        z[:, i, j * P : (j + 1) * P],
+                        ident[:],
+                    )
+            zt_t[q] = banks
+
+        def s_hevac(q):
+            if not valid(q):
+                return
+            ht = work.tile([P, 4, PAIR], BF16, name="ht")
+            for j in range(4):
+                nc.scalar.activation(
+                    out=ht[:, j, :], in_=zt_t[q][j // 2][:, j % 2, :], func=ACT.Relu,
+                    scale=gb1[:, j : j + 1], bias=gb1[:, 4 + j : 5 + j],
+                )
+            ht_t[q] = ht
+            hg = work.tile([P, PAIR, 4], BF16, name="hg", align_bytes=64)
+            hg_t[q] = hg
+
+        def s_regroup(q, half):
+            if not valid(q):
+                return
+            w = slice(half * P, (half + 1) * P)
+            nc.scalar.copy(
+                out=hg_t[q][:, w, :], in_=ht_t[q][:, :, w].rearrange("p j w -> p w j")
+            )
+
+        def v_quant_h(q):
+            if not valid(q):
+                return
+            hq = work.tile([P, PAIR], U32, name="hq", align_bytes=64)
+            hs = work.tile([P, PAIR], U8, name="hs", align_bytes=64)
+            nc.vector.quantize_mx(
+                out=hq[:].bitcast(FP8X4), scales=hs[:],
+                in_=hg_t[q][:].rearrange("p w j -> p (w j)"),
+            )
+            hq_t[q] = (hq, hs)
+
+        def v_gain2(t, q, i):
+            if not valid(q):
+                return
+            if i == 0:
+                a_new = tail.tile([P, 2, D], F32, name="a")
+                a_t[q] = a_new
+            mv = st_t[t][1]
+            nc.vector.scalar_tensor_tensor(
+                out=a_t[q][:, i, :], in0=y2_t[q][i][:], scalar=mv[:, 2 + i, 0:1], in1=g2f[:],
+                op0=ALU.subtract, op1=ALU.mult,
+            )
+
+        def g_finish(t, q, i):
+            if not valid(q):
+                return
+            rr = st_t[t][3]
+            a = a_t[q]
+            nc.gpsimd.tensor_scalar(
+                out=a[:, i, :], in0=a[:, i, :], scalar1=rr[:, 2 + i : 3 + i], scalar2=0.0,
+                op0=ALU.mult, op1=ALU.add,
+            )
+            nc.gpsimd.tensor_tensor(out=a[:, i, :], in0=a[:, i, :], in1=b2f[:], op=ALU.add)
+
+        def store(q):
+            if not valid(q):
+                return
+            nc.sync.dma_start(out=o_pairs[q], in_=a_t[q][:].rearrange("p i d -> p (i d)"))
+
+        for t in range(-2, NPAIR + 2):
+            new_stats(t)
+            s_xevac(t + 1)
+            pe_zt(t - 1)
+            pe_mx(t, xq_t, w1q, w1s, ps_y1, "y1", y1_t)
+            pe_xt(t + 2)
+            s_hevac(t - 1)
+            s_regroup(t - 1, 0)
+            v_stats(t, t - 2, y2_t, 2)
+            v_stats(t, t, y1_t, 0)
+            s_sqrt(t)
+            s_regroup(t - 1, 1)
+            v_quant_x(t + 1)
+            if t == -1:
+                v_prepare_late(0)
+            v_small(t)
+            if t == 0:
+                v_prepare_late(1)
+            s_z1(t)
+            v_gain2(t, t - 2, 0)
+            g_finish(t, t - 2, 0)
+            v_quant_h(t - 1)
+            pe_mx(t - 1, hq_t, w2q, w2s, ps_y2, "y2", y2_t)
+            v_gain2(t, t - 2, 1)
+            g_finish(t, t - 2, 1)
+            store(t - 2)
+            load_x(t + 2 + LOAD_AHEAD)

@@ -18,7 +18,8 @@ PAIR = 2 * P
 NPAIR = TOKENS // PAIR
 EPS = 1e-9
 FLOPS = 2 * 2 * TOKENS * D * D
-LOAD_AHEAD = 6
+LOAD_AHEAD = 8
+LAG2 = 4
 MANUAL = True
 
 
@@ -31,14 +32,14 @@ def tile_rlstmcell_pa_t_kernel(tc, c_att, w1, w2, g1, g2, b1, b2, out):
         if MANUAL:
             ctx.enter_context(tc.manual_schedule())
         const = ctx.enter_context(tc.tile_pool(name="const", bufs=1))
-        xin = ctx.enter_context(tc.tile_pool(name="xin", bufs=LOAD_AHEAD + 3))
+        xin = ctx.enter_context(tc.tile_pool(name="xin", bufs=LOAD_AHEAD + 4))
         work = ctx.enter_context(tc.tile_pool(name="work", bufs=2))
-        tail = ctx.enter_context(tc.tile_pool(name="tail", bufs=3))
-        small = ctx.enter_context(tc.tile_pool(name="small", bufs=3))
+        work3 = ctx.enter_context(tc.tile_pool(name="work3", bufs=3))
+        work4 = ctx.enter_context(tc.tile_pool(name="work4", bufs=4))
         ps_xt = ctx.enter_context(tc.psum_pool(name="ps_xt", bufs=1))
-        ps_y1 = ctx.enter_context(tc.psum_pool(name="ps_y1", bufs=2))
+        ps_y1 = ctx.enter_context(tc.psum_pool(name="ps_y1", bufs=3))
         ps_zt = ctx.enter_context(tc.psum_pool(name="ps_zt", bufs=2))
-        ps_y2 = ctx.enter_context(tc.psum_pool(name="ps_y2", bufs=3))
+        ps_y2 = ctx.enter_context(tc.psum_pool(name="ps_y2", bufs=2))
 
         x_t = {}
         xt_t = {}
@@ -52,7 +53,9 @@ def tile_rlstmcell_pa_t_kernel(tc, c_att, w1, w2, g1, g2, b1, b2, out):
         hq_t = {}
         y2_t = {}
         a_t = {}
-        st_t = {}
+        st1_t = {}
+        st2_t = {}
+        tick_t = {}
 
         def valid(q):
             return 0 <= q < NPAIR
@@ -68,13 +71,13 @@ def tile_rlstmcell_pa_t_kernel(tc, c_att, w1, w2, g1, g2, b1, b2, out):
             load_x(q)
         gbr = const.tile([P, P], BF16, name="gbr")
         nc.vector.memset(gbr[:], 0.0)
-        nc.scalar.dma_start(out=gbr[0:4, :], in_=g1.rearrange("(j p) -> j p", p=P))
-        nc.scalar.dma_start(out=gbr[4:8, :], in_=b1.rearrange("(j p) -> j p", p=P))
         w1raw = const.tile([P, 4, D], BF16, name="w1raw")
         nc.scalar.dma_start(
             out=w1raw[:].rearrange("p (u e) n -> p u (e n)", u=2),
             in_=w1.rearrange("(u p e) n -> p u (e n)", u=2, e=2),
         )
+        nc.scalar.dma_start(out=gbr[0:4, :], in_=g1.rearrange("(j p) -> j p", p=P))
+        nc.scalar.dma_start(out=gbr[4:8, :], in_=b1.rearrange("(j p) -> j p", p=P))
         w2raw = const.tile([P, 4, D], BF16, name="w2raw")
         nc.scalar.dma_start(out=w2raw[:], in_=w2.rearrange("(t p) n -> p t n", p=P))
         g2b = const.tile([P, D], BF16, name="g2b")
@@ -91,13 +94,6 @@ def tile_rlstmcell_pa_t_kernel(tc, c_att, w1, w2, g1, g2, b1, b2, out):
         ident = const.tile([P, P], F32, name="ident")
         make_identity(nc, ident[:])
 
-        gbf = const.tile([P, P], F32, name="gbf")
-        nc.vector.tensor_copy(out=gbf[:], in_=gbr[:])
-        gbt = ps_zt.tile([P, 2, PAIR], F32, name="zt")
-        nc.tensor.transpose(gbt[:, 0, 0:P], gbf[:], ident[:])
-        gb1 = const.tile([P, 8], F32, name="gb1")
-        nc.vector.tensor_copy(out=gb1[:], in_=gbt[:, 0, 0:8])
-
         w1g = const.tile([P, D, 4], BF16, name="w1g", align_bytes=64)
         w1q = const.tile([P, D], U32, name="w1q", align_bytes=64)
         w1s = const.tile([P, D], U8, name="w1s", align_bytes=64)
@@ -106,13 +102,19 @@ def tile_rlstmcell_pa_t_kernel(tc, c_att, w1, w2, g1, g2, b1, b2, out):
         w2s = const.tile([P, D], U8, name="w2s", align_bytes=64)
         g2f = const.tile([P, D], F32, name="g2f")
         b2f = const.tile([P, D], F32, name="b2f")
+        gbf = const.tile([P, P], F32, name="gbf")
+        gb1 = const.tile([P, 8], F32, name="gb1")
         nc.vector.tensor_copy(out=w1g[:], in_=w1raw[:].rearrange("p t n -> p n t"))
         nc.vector.quantize_mx(
             out=w1q[:].bitcast(FP8X4), scales=w1s[:], in_=w1g[:].rearrange("p n t -> p (n t)")
         )
 
-        def v_prepare_late(step):
+        def prepare_late(step):
             if step == 0:
+                nc.vector.tensor_copy(out=gbf[:], in_=gbr[:])
+                gbt = ps_zt.tile([P, 2, PAIR], F32, name="zt")
+                nc.tensor.transpose(gbt[:, 0, 0:P], gbf[:], ident[:])
+                nc.vector.tensor_copy(out=gb1[:], in_=gbt[:, 0, 0:8])
                 nc.vector.tensor_copy(out=w2g[:], in_=w2raw[:].rearrange("p t n -> p n t"))
             else:
                 nc.vector.quantize_mx(
@@ -146,123 +148,149 @@ def tile_rlstmcell_pa_t_kernel(tc, c_att, w1, w2, g1, g2, b1, b2, out):
         def v_quant_x(q):
             if not valid(q):
                 return
-            xq = work.tile([P, PAIR], U32, name="xq", align_bytes=64)
-            xs = work.tile([P, PAIR], U8, name="xs", align_bytes=64)
+            xq = work3.tile([P, PAIR], U32, name="xq", align_bytes=64)
+            xs = work3.tile([P, PAIR], U8, name="xs", align_bytes=64)
             nc.vector.quantize_mx(out=xq[:].bitcast(FP8X4), scales=xs[:], in_=xg_t[q][:])
             xq_t[q] = (xq, xs)
 
-        def pe_mx(q, src, wq, ws, pool, nm, dst):
+        def pe_mx(q, i, src, wq, ws, pool, nm, dst):
             if not valid(q):
                 return
             codes, scales = src[q]
-            banks = []
-            for i in range(2):
-                acc = pool.tile([P, D], F32, name=nm)
-                cols = slice(i * P, (i + 1) * P)
-                nc.tensor.matmul_mx(
-                    out=acc[:],
-                    lhsT=codes[:, cols].bitcast(FP8X4),
-                    lhsT_scale=scales[:, cols],
-                    rhs=wq[:].bitcast(FP8X4),
-                    rhs_scale=ws[:],
-                    start=True,
-                    stop=True,
-                )
-                banks.append(acc)
-            dst[q] = banks
+            acc = pool.tile([P, D], F32, name=nm)
+            cols = slice(i * P, (i + 1) * P)
+            nc.tensor.matmul_mx(
+                out=acc[:],
+                lhsT=codes[:, cols].bitcast(FP8X4),
+                lhsT_scale=scales[:, cols],
+                rhs=wq[:].bitcast(FP8X4),
+                rhs_scale=ws[:],
+                start=True,
+                stop=True,
+            )
+            dst[(q, i)] = acc
 
-        def span(t):
-            lo = 0 if valid(t) else 2
-            hi = 4 if valid(t - 2) else 2
+        def pe_mx1(q, i):
+            pe_mx(q, i, xq_t, w1q, w1s, ps_y1, "y1", y1_t)
+
+        def pe_mx2(q, i):
+            pe_mx(q, i, hq_t, w2q, w2s, ps_y2, "y2", y2_t)
+
+        def span(T):
+            lo = 0 if valid(T) else 2
+            hi = 4 if valid(T - LAG2) else 2
             return lo, hi
 
-        def new_stats(t):
-            lo, hi = span(t)
+        def new_set(T):
+            lo, hi = span(T)
             if lo >= hi:
                 return
-            st = small.tile([P, 4, 6], F32, name="st")
-            mv = small.tile([P, 4, 2], F32, name="mv")
-            sd = small.tile([P, 4], F32, name="sd")
-            rr = small.tile([P, 4], F32, name="rr")
+            mv = work4.tile([P, 4, 2], F32, name="mv")
+            sd = work4.tile([P, 4], F32, name="sd")
+            rr = work4.tile([P, 4], F32, name="rr")
             nmr = None
-            if valid(t):
-                nmr = small.tile([P, 2], F32, name="nmr")
-            st_t[t] = (st, mv, sd, rr, nmr)
+            if valid(T):
+                nmr = work4.tile([P, 2], F32, name="nmr")
+            tick_t[T] = (mv, sd, rr, nmr)
 
-        def v_stats(t, q, banks, base):
+        def v_bn1(q, i):
             if not valid(q):
                 return
-            st, mv = st_t[t][0], st_t[t][1]
-            for i in range(2):
-                nc.vector.bn_stats(out=st[:, base + i, :], in_=banks[q][i][:])
-            for i in range(2):
-                nc.vector.bn_aggr(out=mv[:, base + i, :], in_=st[:, base + i, :])
+            if i == 0:
+                st1 = work.tile([P, 2, 6], F32, name="st1")
+                st1_t[q] = st1
+            nc.vector.bn_stats(out=st1_t[q][:, i, :], in_=y1_t[(q, i)][:])
 
-        def s_sqrt(t):
-            lo, hi = span(t)
+        def v_ag1(q, i):
+            if not valid(q):
+                return
+            nc.vector.bn_aggr(out=tick_t[q][0][:, i, :], in_=st1_t[q][:, i, :])
+
+        def v_bn2(q, i):
+            if not valid(q):
+                return
+            if i == 0:
+                st2 = work3.tile([P, 2, 6], F32, name="st2")
+                st2_t[q] = st2
+            nc.vector.bn_stats(out=st2_t[q][:, i, :], in_=y2_t[(q, i)][:])
+
+        def v_ag2(q, i):
+            if not valid(q):
+                return
+            nc.vector.bn_aggr(out=tick_t[q + LAG2][0][:, 2 + i, :], in_=st2_t[q][:, i, :])
+
+        def s_sqrt(T, q, base):
+            if not valid(q):
+                return
+            mv, sd = tick_t[T][0], tick_t[T][1]
+            nc.scalar.activation(
+                out=sd[:, base : base + 2], in_=mv[:, base : base + 2, 1], func=ACT.Sqrt
+            )
+
+        def v_eps(T):
+            lo, hi = span(T)
             if lo >= hi:
                 return
-            mv, sd = st_t[t][1], st_t[t][2]
-            nc.scalar.activation(out=sd[:, lo:hi], in_=mv[:, lo:hi, 1], func=ACT.Sqrt)
-
-        def v_small(t):
-            lo, hi = span(t)
-            if lo >= hi:
-                return
-            st, mv, sd, rr, nmr = st_t[t]
+            sd = tick_t[T][1]
             nc.vector.tensor_scalar_add(out=sd[:, lo:hi], in0=sd[:, lo:hi], scalar1=EPS)
-            nc.vector.reciprocal(out=rr[:, lo:hi], in_=sd[:, lo:hi])
-            if valid(t):
-                nc.vector.scalar_tensor_tensor(
-                    out=nmr[:], in0=mv[:, 0:2, 0], scalar=-1.0, in1=rr[:, 0:2],
-                    op0=ALU.mult, op1=ALU.mult,
-                )
 
-        def s_z1(q):
+        def v_recip(T):
+            lo, hi = span(T)
+            if lo >= hi:
+                return
+            nc.vector.reciprocal(out=tick_t[T][2][:, lo:hi], in_=tick_t[T][1][:, lo:hi])
+
+        def v_nmr(T):
+            if not valid(T):
+                return
+            mv, sd, rr, nmr = tick_t[T]
+            nc.vector.scalar_tensor_tensor(
+                out=nmr[:], in0=mv[:, 0:2, 0], scalar=-1.0, in1=rr[:, 0:2],
+                op0=ALU.mult, op1=ALU.mult,
+            )
+
+        def s_z1(q, i):
             if not valid(q):
                 return
-            rr, nmr = st_t[q][3], st_t[q][4]
-            z = work.tile([P, 2, D], F32, name="z")
-            for i in range(2):
-                nc.scalar.activation(
-                    out=z[:, i, :], in_=y1_t[q][i][:], func=ACT.Identity,
-                    scale=rr[:, i : i + 1], bias=nmr[:, i : i + 1],
-                )
-            z_t[q] = z
+            rr, nmr = tick_t[q][2], tick_t[q][3]
+            if i == 0:
+                z_new = work3.tile([P, 2, D], F32, name="z")
+                z_t[q] = z_new
+            nc.scalar.activation(
+                out=z_t[q][:, i, :], in_=y1_t[(q, i)][:], func=ACT.Identity,
+                scale=rr[:, i : i + 1], bias=nmr[:, i : i + 1],
+            )
 
-        def pe_zt(q):
+        def pe_zt(q, h):
             if not valid(q):
                 return
             z = z_t[q]
-            banks = []
-            for h in range(2):
-                zt = ps_zt.tile([P, 2, PAIR], F32, name="zt")
-                banks.append(zt)
-            for i in range(2):
-                for j in range(4):
+            zt = ps_zt.tile([P, 2, PAIR], F32, name="zt")
+            for jj in range(2):
+                j = 2 * h + jj
+                for i in range(2):
                     nc.tensor.transpose(
-                        banks[j // 2][:, j % 2, i * P : (i + 1) * P],
-                        z[:, i, j * P : (j + 1) * P],
-                        ident[:],
+                        zt[:, jj, i * P : (i + 1) * P], z[:, i, j * P : (j + 1) * P], ident[:]
                     )
-            zt_t[q] = banks
+            zt_t[(q, h)] = zt
 
-        def s_hevac(q):
+        def s_hevac(q, j):
             if not valid(q):
                 return
-            ht = work.tile([P, 4, PAIR], BF16, name="ht")
-            for j in range(4):
-                nc.scalar.activation(
-                    out=ht[:, j, :], in_=zt_t[q][j // 2][:, j % 2, :], func=ACT.Relu,
-                    scale=gb1[:, j : j + 1], bias=gb1[:, 4 + j : 5 + j],
-                )
-            ht_t[q] = ht
-            hg = work.tile([P, PAIR, 4], BF16, name="hg", align_bytes=64)
-            hg_t[q] = hg
+            if q not in ht_t:
+                ht_new = work3.tile([P, 4, PAIR], BF16, name="ht")
+                ht_t[q] = ht_new
+            nc.scalar.activation(
+                out=ht_t[q][:, j, :], in_=zt_t[(q, j // 2)][:, j % 2, :], func=ACT.Relu,
+                scale=gb1[:, j : j + 1], bias=gb1[:, 4 + j : 5 + j],
+            )
 
         def s_regroup(q, half):
             if not valid(q):
                 return
+            if half == 0:
+                hg_new = work3.tile([P, PAIR, 4], BF16, name="hg", align_bytes=64)
+                hg_t[q] = hg_new
             w = slice(half * P, (half + 1) * P)
             nc.scalar.copy(
                 out=hg_t[q][:, w, :], in_=ht_t[q][:, :, w].rearrange("p j w -> p w j")
@@ -279,27 +307,32 @@ def tile_rlstmcell_pa_t_kernel(tc, c_att, w1, w2, g1, g2, b1, b2, out):
             )
             hq_t[q] = (hq, hs)
 
-        def v_gain2(t, q, i):
+        def v_gain2(q, i):
             if not valid(q):
                 return
             if i == 0:
-                a_new = tail.tile([P, 2, D], F32, name="a")
+                a_new = work4.tile([P, 2, D], F32, name="a")
                 a_t[q] = a_new
-            mv = st_t[t][1]
+            mv = tick_t[q + LAG2][0]
             nc.vector.scalar_tensor_tensor(
-                out=a_t[q][:, i, :], in0=y2_t[q][i][:], scalar=mv[:, 2 + i, 0:1], in1=g2f[:],
+                out=a_t[q][:, i, :], in0=y2_t[(q, i)][:], scalar=mv[:, 2 + i, 0:1], in1=g2f[:],
                 op0=ALU.subtract, op1=ALU.mult,
             )
 
-        def g_finish(t, q, i):
+        def g_scale(q, i):
             if not valid(q):
                 return
-            rr = st_t[t][3]
+            rr = tick_t[q + LAG2][2]
             a = a_t[q]
             nc.gpsimd.tensor_scalar(
                 out=a[:, i, :], in0=a[:, i, :], scalar1=rr[:, 2 + i : 3 + i], scalar2=0.0,
                 op0=ALU.mult, op1=ALU.add,
             )
+
+        def g_bias(q, i):
+            if not valid(q):
+                return
+            a = a_t[q]
             nc.gpsimd.tensor_tensor(out=a[:, i, :], in0=a[:, i, :], in1=b2f[:], op=ALU.add)
 
         def store(q):
@@ -307,30 +340,48 @@ def tile_rlstmcell_pa_t_kernel(tc, c_att, w1, w2, g1, g2, b1, b2, out):
                 return
             nc.sync.dma_start(out=o_pairs[q], in_=a_t[q][:].rearrange("p i d -> p (i d)"))
 
-        for t in range(-2, NPAIR + 2):
-            new_stats(t)
-            s_xevac(t + 1)
-            pe_zt(t - 1)
-            pe_mx(t, xq_t, w1q, w1s, ps_y1, "y1", y1_t)
-            pe_xt(t + 2)
-            s_hevac(t - 1)
-            s_regroup(t - 1, 0)
-            v_stats(t, t - 2, y2_t, 2)
-            v_stats(t, t, y1_t, 0)
-            s_sqrt(t)
-            s_regroup(t - 1, 1)
-            v_quant_x(t + 1)
+        for t in range(-3, NPAIR + 4):
+            new_set(t + 1)
+            v_eps(t)
+            v_quant_x(t + 2)
+            if t == -2:
+                prepare_late(0)
             if t == -1:
-                v_prepare_late(0)
-            v_small(t)
-            if t == 0:
-                v_prepare_late(1)
-            s_z1(t)
-            v_gain2(t, t - 2, 0)
-            g_finish(t, t - 2, 0)
-            v_quant_h(t - 1)
-            pe_mx(t - 1, hq_t, w2q, w2s, ps_y2, "y2", y2_t)
-            v_gain2(t, t - 2, 1)
-            g_finish(t, t - 2, 1)
-            store(t - 2)
-            load_x(t + 2 + LOAD_AHEAD)
+                prepare_late(1)
+            pe_zt(t - 1, 1)
+            s_regroup(t - 2, 1)
+            v_recip(t)
+            v_ag2(t - 3, 0)
+            v_ag2(t - 3, 1)
+            pe_xt(t + 3)
+            v_nmr(t)
+            g_scale(t - 4, 0)
+            v_gain2(t - 3, 0)
+            s_z1(t, 0)
+            v_quant_h(t - 2)
+            g_scale(t - 4, 1)
+            v_bn1(t + 1, 0)
+            s_hevac(t - 1, 2)
+            s_hevac(t - 1, 3)
+            pe_mx1(t + 1, 1)
+            g_bias(t - 4, 0)
+            v_gain2(t - 3, 1)
+            s_hevac(t - 1, 0)
+            pe_mx2(t - 2, 0)
+            s_z1(t, 1)
+            v_ag1(t + 1, 0)
+            v_bn1(t + 1, 1)
+            s_xevac(t + 3)
+            pe_mx2(t - 2, 1)
+            g_bias(t - 4, 1)
+            v_bn2(t - 2, 0)
+            pe_mx1(t + 2, 0)
+            s_hevac(t - 1, 1)
+            s_sqrt(t + 1, t - 3, 2)
+            v_ag1(t + 1, 1)
+            v_bn2(t - 2, 1)
+            pe_zt(t, 0)
+            s_sqrt(t + 1, t + 1, 0)
+            s_regroup(t - 1, 0)
+            store(t - 4)
+            load_x(t + 3 + LOAD_AHEAD)

@@ -18,9 +18,9 @@ PAIR = 2 * P
 NPAIR = TOKENS // PAIR
 EPS = 1e-9
 FLOPS = 2 * 2 * TOKENS * D * D
-LOAD_AHEAD = 8
 LAG2 = 4
-MANUAL = True
+FIRST_LOADS = 6
+VECTOR_TAIL = (30, 31)
 
 
 def tile_rlstmcell_pa_t_kernel(tc, c_att, w1, w2, g1, g2, b1, b2, out):
@@ -29,16 +29,13 @@ def tile_rlstmcell_pa_t_kernel(tc, c_att, w1, w2, g1, g2, b1, b2, out):
     o_pairs = out.flatten_outer_dims().rearrange("(q p i) d -> q p (i d)", p=P, i=2)
 
     with ExitStack() as ctx:
-        if MANUAL:
-            ctx.enter_context(tc.manual_schedule())
+        ctx.enter_context(tc.manual_schedule())
         const = ctx.enter_context(tc.tile_pool(name="const", bufs=1))
-        xin = ctx.enter_context(tc.tile_pool(name="xin", bufs=LOAD_AHEAD + 4))
-        work = ctx.enter_context(tc.tile_pool(name="work", bufs=2))
+        xin = ctx.enter_context(tc.tile_pool(name="xin", bufs=FIRST_LOADS + 3))
         work3 = ctx.enter_context(tc.tile_pool(name="work3", bufs=3))
-        work4 = ctx.enter_context(tc.tile_pool(name="work4", bufs=4))
-        ps_xt = ctx.enter_context(tc.psum_pool(name="ps_xt", bufs=1))
-        ps_y1 = ctx.enter_context(tc.psum_pool(name="ps_y1", bufs=3))
-        ps_zt = ctx.enter_context(tc.psum_pool(name="ps_zt", bufs=2))
+        work6 = ctx.enter_context(tc.tile_pool(name="work6", bufs=6))
+        ps_tp = ctx.enter_context(tc.psum_pool(name="ps_tp", bufs=2))
+        ps_y1 = ctx.enter_context(tc.psum_pool(name="ps_y1", bufs=4))
         ps_y2 = ctx.enter_context(tc.psum_pool(name="ps_y2", bufs=2))
 
         x_t = {}
@@ -55,7 +52,7 @@ def tile_rlstmcell_pa_t_kernel(tc, c_att, w1, w2, g1, g2, b1, b2, out):
         a_t = {}
         st1_t = {}
         st2_t = {}
-        tick_t = {}
+        set_t = {}
 
         def valid(q):
             return 0 <= q < NPAIR
@@ -84,12 +81,14 @@ def tile_rlstmcell_pa_t_kernel(tc, c_att, w1, w2, g1, g2, b1, b2, out):
         nc.scalar.dma_start(out=g2b[:], in_=g2.partition_broadcast(P))
         b2b = const.tile([P, D], BF16, name="b2b")
         nc.scalar.dma_start(out=b2b[:], in_=b2.partition_broadcast(P))
-        for q in range(2, LOAD_AHEAD):
+        for q in range(2, FIRST_LOADS):
             load_x(q)
 
         one = const.tile([P, 1], F32, name="one")
         nc.vector.memset(one[:], 1.0)
         nc.scalar.activation(out=one[:], in_=one[:], func=ACT.Sqrt)
+        epsc = const.tile([P, 1], F32, name="epsc")
+        nc.vector.memset(epsc[:], EPS)
 
         ident = const.tile([P, P], F32, name="ident")
         make_identity(nc, ident[:])
@@ -112,7 +111,7 @@ def tile_rlstmcell_pa_t_kernel(tc, c_att, w1, w2, g1, g2, b1, b2, out):
         def prepare_late(step):
             if step == 0:
                 nc.vector.tensor_copy(out=gbf[:], in_=gbr[:])
-                gbt = ps_zt.tile([P, 2, PAIR], F32, name="zt")
+                gbt = ps_tp.tile([P, 2, PAIR], F32, name="gbt", tag="tp")
                 nc.tensor.transpose(gbt[:, 0, 0:P], gbf[:], ident[:])
                 nc.vector.tensor_copy(out=gb1[:], in_=gbt[:, 0, 0:8])
                 nc.vector.tensor_copy(out=w2g[:], in_=w2raw[:].rearrange("p t n -> p n t"))
@@ -127,7 +126,7 @@ def tile_rlstmcell_pa_t_kernel(tc, c_att, w1, w2, g1, g2, b1, b2, out):
         def pe_xt(q):
             if not valid(q):
                 return
-            xt = ps_xt.tile([P, 2, 2, P], F32, name="xt")
+            xt = ps_tp.tile([P, 2, 2, P], F32, name="xt", tag="tp")
             x32 = x_t[q][:].bitcast(F32)
             for i in range(2):
                 for u in range(2):
@@ -138,7 +137,7 @@ def tile_rlstmcell_pa_t_kernel(tc, c_att, w1, w2, g1, g2, b1, b2, out):
         def s_xevac(q):
             if not valid(q):
                 return
-            xg = work.tile([P, 4 * PAIR], BF16, name="xg", align_bytes=64)
+            xg = work3.tile([P, 4 * PAIR], BF16, name="xg", align_bytes=64)
             nc.scalar.copy(
                 out=xg[:].bitcast(F32).rearrange("p (i w u) -> p i w u", i=2, u=2),
                 in_=xt_t[q][:].rearrange("p i u w -> p i w u"),
@@ -176,35 +175,31 @@ def tile_rlstmcell_pa_t_kernel(tc, c_att, w1, w2, g1, g2, b1, b2, out):
         def pe_mx2(q, i):
             pe_mx(q, i, hq_t, w2q, w2s, ps_y2, "y2", y2_t)
 
-        def span(T):
-            lo = 0 if valid(T) else 2
-            hi = 4 if valid(T - LAG2) else 2
+        def span(s):
+            lo = 0 if valid(s) else 2
+            hi = 4 if valid(s - LAG2) else 2
             return lo, hi
 
-        def new_set(T):
-            lo, hi = span(T)
-            if lo >= hi:
-                return
-            mv = work4.tile([P, 4, 2], F32, name="mv")
-            sd = work4.tile([P, 4], F32, name="sd")
-            rr = work4.tile([P, 4], F32, name="rr")
-            nmr = None
-            if valid(T):
-                nmr = work4.tile([P, 2], F32, name="nmr")
-            tick_t[T] = (mv, sd, rr, nmr)
+        def small_set(s):
+            if s not in set_t:
+                mv = work6.tile([P, 4, 2], F32, name="mv")
+                sd = work6.tile([P, 4], F32, name="sd")
+                rr = work6.tile([P, 4], F32, name="rr")
+                set_t[s] = (mv, sd, rr)
+            return set_t[s]
 
         def v_bn1(q, i):
             if not valid(q):
                 return
             if i == 0:
-                st1 = work.tile([P, 2, 6], F32, name="st1")
+                st1 = work3.tile([P, 2, 6], F32, name="st1")
                 st1_t[q] = st1
             nc.vector.bn_stats(out=st1_t[q][:, i, :], in_=y1_t[(q, i)][:])
 
         def v_ag1(q, i):
             if not valid(q):
                 return
-            nc.vector.bn_aggr(out=tick_t[q][0][:, i, :], in_=st1_t[q][:, i, :])
+            nc.vector.bn_aggr(out=small_set(q)[0][:, i, :], in_=st1_t[q][:, i, :])
 
         def v_bn2(q, i):
             if not valid(q):
@@ -217,55 +212,74 @@ def tile_rlstmcell_pa_t_kernel(tc, c_att, w1, w2, g1, g2, b1, b2, out):
         def v_ag2(q, i):
             if not valid(q):
                 return
-            nc.vector.bn_aggr(out=tick_t[q + LAG2][0][:, 2 + i, :], in_=st2_t[q][:, i, :])
+            nc.vector.bn_aggr(out=small_set(q + LAG2)[0][:, 2 + i, :], in_=st2_t[q][:, i, :])
 
-        def s_sqrt(T, q, base):
-            if not valid(q):
-                return
-            mv, sd = tick_t[T][0], tick_t[T][1]
+        def s_sqrt(s, base):
+            mv, sd, rr = small_set(s)
             nc.scalar.activation(
                 out=sd[:, base : base + 2], in_=mv[:, base : base + 2, 1], func=ACT.Sqrt
             )
 
-        def v_eps(T):
-            lo, hi = span(T)
+        def s_sqrt1(q):
+            if valid(q):
+                s_sqrt(q, 0)
+
+        def s_sqrt2(q):
+            if valid(q):
+                s_sqrt(q + LAG2, 2)
+
+        nm_t = {}
+        nmr_t = {}
+
+        def s_negmean(q):
+            if not valid(q):
+                return
+            nm = work3.tile([P, 2], F32, name="nm")
+            nc.scalar.mul(out=nm[:], in_=small_set(q)[0][:, 0:2, 0], mul=-1.0)
+            nm_t[q] = nm
+
+        def s_eps(s):
+            lo, hi = span(s)
             if lo >= hi:
                 return
-            sd = tick_t[T][1]
-            nc.vector.tensor_scalar_add(out=sd[:, lo:hi], in0=sd[:, lo:hi], scalar1=EPS)
-
-        def v_recip(T):
-            lo, hi = span(T)
-            if lo >= hi:
-                return
-            nc.vector.reciprocal(out=tick_t[T][2][:, lo:hi], in_=tick_t[T][1][:, lo:hi])
-
-        def v_nmr(T):
-            if not valid(T):
-                return
-            mv, sd, rr, nmr = tick_t[T]
-            nc.vector.scalar_tensor_tensor(
-                out=nmr[:], in0=mv[:, 0:2, 0], scalar=-1.0, in1=rr[:, 0:2],
-                op0=ALU.mult, op1=ALU.mult,
+            sd = small_set(s)[1]
+            nc.scalar.activation(
+                out=sd[:, lo:hi], in_=sd[:, lo:hi], func=ACT.Identity, bias=epsc[:, 0:1]
             )
+
+        def v_recip(s):
+            lo, hi = span(s)
+            if lo >= hi:
+                return
+            mv, sd, rr = small_set(s)
+            nc.vector.reciprocal(out=rr[:, lo:hi], in_=sd[:, lo:hi])
+
+        def g_negmean_r(q):
+            if not valid(q):
+                return
+            nmr = work3.tile([P, 2], F32, name="nmr")
+            nc.gpsimd.tensor_tensor(
+                out=nmr[:], in0=nm_t[q][:], in1=small_set(q)[2][:, 0:2], op=ALU.mult
+            )
+            nmr_t[q] = nmr
 
         def s_z1(q, i):
             if not valid(q):
                 return
-            rr, nmr = tick_t[q][2], tick_t[q][3]
+            rr = small_set(q)[2]
             if i == 0:
                 z_new = work3.tile([P, 2, D], F32, name="z")
                 z_t[q] = z_new
             nc.scalar.activation(
                 out=z_t[q][:, i, :], in_=y1_t[(q, i)][:], func=ACT.Identity,
-                scale=rr[:, i : i + 1], bias=nmr[:, i : i + 1],
+                scale=rr[:, i : i + 1], bias=nmr_t[q][:, i : i + 1],
             )
 
         def pe_zt(q, h):
             if not valid(q):
                 return
             z = z_t[q]
-            zt = ps_zt.tile([P, 2, PAIR], F32, name="zt")
+            zt = ps_tp.tile([P, 2, PAIR], F32, name="zt", tag="tp")
             for jj in range(2):
                 j = 2 * h + jj
                 for i in range(2):
@@ -299,8 +313,8 @@ def tile_rlstmcell_pa_t_kernel(tc, c_att, w1, w2, g1, g2, b1, b2, out):
         def v_quant_h(q):
             if not valid(q):
                 return
-            hq = work.tile([P, PAIR], U32, name="hq", align_bytes=64)
-            hs = work.tile([P, PAIR], U8, name="hs", align_bytes=64)
+            hq = work3.tile([P, PAIR], U32, name="hq", align_bytes=64)
+            hs = work3.tile([P, PAIR], U8, name="hs", align_bytes=64)
             nc.vector.quantize_mx(
                 out=hq[:].bitcast(FP8X4), scales=hs[:],
                 in_=hg_t[q][:].rearrange("p w j -> p (w j)"),
@@ -310,19 +324,29 @@ def tile_rlstmcell_pa_t_kernel(tc, c_att, w1, w2, g1, g2, b1, b2, out):
         def v_gain2(q, i):
             if not valid(q):
                 return
-            if i == 0:
-                a_new = work4.tile([P, 2, D], F32, name="a")
+            if q not in a_t:
+                a_new = work6.tile([P, 2, D], F32, name="a")
                 a_t[q] = a_new
-            mv = tick_t[q + LAG2][0]
+            mv = small_set(q + LAG2)[0]
             nc.vector.scalar_tensor_tensor(
                 out=a_t[q][:, i, :], in0=y2_t[(q, i)][:], scalar=mv[:, 2 + i, 0:1], in1=g2f[:],
                 op0=ALU.subtract, op1=ALU.mult,
             )
 
-        def g_scale(q, i):
-            if not valid(q):
+        def v_finish(q, i):
+            if not valid(q) or q not in VECTOR_TAIL:
                 return
-            rr = tick_t[q + LAG2][2]
+            rr = small_set(q + LAG2)[2]
+            a = a_t[q]
+            nc.vector.scalar_tensor_tensor(
+                out=a[:, i, :], in0=a[:, i, :], scalar=rr[:, 2 + i : 3 + i], in1=b2f[:],
+                op0=ALU.mult, op1=ALU.add,
+            )
+
+        def g_scale(q, i):
+            if not valid(q) or q in VECTOR_TAIL:
+                return
+            rr = small_set(q + LAG2)[2]
             a = a_t[q]
             nc.gpsimd.tensor_scalar(
                 out=a[:, i, :], in0=a[:, i, :], scalar1=rr[:, 2 + i : 3 + i], scalar2=0.0,
@@ -330,7 +354,7 @@ def tile_rlstmcell_pa_t_kernel(tc, c_att, w1, w2, g1, g2, b1, b2, out):
             )
 
         def g_bias(q, i):
-            if not valid(q):
+            if not valid(q) or q in VECTOR_TAIL:
                 return
             a = a_t[q]
             nc.gpsimd.tensor_tensor(out=a[:, i, :], in0=a[:, i, :], in1=b2f[:], op=ALU.add)
@@ -340,48 +364,50 @@ def tile_rlstmcell_pa_t_kernel(tc, c_att, w1, w2, g1, g2, b1, b2, out):
                 return
             nc.sync.dma_start(out=o_pairs[q], in_=a_t[q][:].rearrange("p i d -> p (i d)"))
 
-        for t in range(-3, NPAIR + 4):
-            new_set(t + 1)
-            v_eps(t)
+        for t in range(-3, NPAIR + 6):
+            v_recip(t)
+            v_finish(t - 4, 0)
+            pe_zt(t - 1, 1)
+            v_bn1(t + 1, 0)
+            s_negmean(t)
+            pe_mx1(t + 1, 1)
+            s_hevac(t - 1, 0)
+            g_scale(t - 4, 1)
+            v_ag2(t - 3, 1)
+            v_gain2(t - 3, 0)
+            v_finish(t - 4, 1)
+            store(t - 6)
+            s_hevac(t - 1, 1)
+            load_x(t + 9)
+            s_sqrt2(t - 3)
+            s_hevac(t - 1, 3)
+            g_negmean_r(t)
+            v_quant_h(t - 2)
+            s_hevac(t - 1, 2)
+            pe_xt(t + 3)
+            g_bias(t - 4, 1)
+            v_gain2(t - 3, 1)
+            s_z1(t, 0)
+            pe_mx2(t - 2, 0)
+            v_bn1(t + 1, 1)
+            s_z1(t, 1)
+            pe_mx2(t - 2, 1)
+            s_regroup(t - 1, 0)
             v_quant_x(t + 2)
             if t == -2:
                 prepare_late(0)
             if t == -1:
                 prepare_late(1)
-            pe_zt(t - 1, 1)
-            s_regroup(t - 2, 1)
-            v_recip(t)
-            v_ag2(t - 3, 0)
-            v_ag2(t - 3, 1)
-            pe_xt(t + 3)
-            v_nmr(t)
             g_scale(t - 4, 0)
-            v_gain2(t - 3, 0)
-            s_z1(t, 0)
-            v_quant_h(t - 2)
-            g_scale(t - 4, 1)
-            v_bn1(t + 1, 0)
-            s_hevac(t - 1, 2)
-            s_hevac(t - 1, 3)
-            pe_mx1(t + 1, 1)
-            g_bias(t - 4, 0)
-            v_gain2(t - 3, 1)
-            s_hevac(t - 1, 0)
-            pe_mx2(t - 2, 0)
-            s_z1(t, 1)
             v_ag1(t + 1, 0)
-            v_bn1(t + 1, 1)
-            s_xevac(t + 3)
-            pe_mx2(t - 2, 1)
-            g_bias(t - 4, 1)
+            v_ag1(t + 1, 1)
             v_bn2(t - 2, 0)
             pe_mx1(t + 2, 0)
-            s_hevac(t - 1, 1)
-            s_sqrt(t + 1, t - 3, 2)
-            v_ag1(t + 1, 1)
-            v_bn2(t - 2, 1)
+            s_sqrt1(t + 1)
+            s_xevac(t + 3)
             pe_zt(t, 0)
-            s_sqrt(t + 1, t + 1, 0)
-            s_regroup(t - 1, 0)
-            store(t - 4)
-            load_x(t + 3 + LOAD_AHEAD)
+            v_bn2(t - 2, 1)
+            g_bias(t - 5, 0)
+            s_eps(t + 1)
+            s_regroup(t - 1, 1)
+            v_ag2(t - 2, 0)

@@ -19,7 +19,7 @@ NPAIR = TOKENS // PAIR
 EPS = 1e-9
 FLOPS = 2 * 2 * TOKENS * D * D
 LAG2 = 4
-FIRST_LOADS = 6
+FIRST_LOADS = 7
 VECTOR_TAIL = (30, 31)
 
 
@@ -87,8 +87,6 @@ def tile_rlstmcell_pa_t_kernel(tc, c_att, w1, w2, g1, g2, b1, b2, out):
         one = const.tile([P, 1], F32, name="one")
         nc.vector.memset(one[:], 1.0)
         nc.scalar.activation(out=one[:], in_=one[:], func=ACT.Sqrt)
-        epsc = const.tile([P, 1], F32, name="epsc")
-        nc.vector.memset(epsc[:], EPS)
 
         ident = const.tile([P, P], F32, name="ident")
         make_identity(nc, ident[:])
@@ -214,19 +212,12 @@ def tile_rlstmcell_pa_t_kernel(tc, c_att, w1, w2, g1, g2, b1, b2, out):
                 return
             nc.vector.bn_aggr(out=small_set(q + LAG2)[0][:, 2 + i, :], in_=st2_t[q][:, i, :])
 
-        def s_sqrt(s, base):
+        def s_sqrt(s):
+            lo, hi = span(s)
+            if lo >= hi:
+                return
             mv, sd, rr = small_set(s)
-            nc.scalar.activation(
-                out=sd[:, base : base + 2], in_=mv[:, base : base + 2, 1], func=ACT.Sqrt
-            )
-
-        def s_sqrt1(q):
-            if valid(q):
-                s_sqrt(q, 0)
-
-        def s_sqrt2(q):
-            if valid(q):
-                s_sqrt(q + LAG2, 2)
+            nc.scalar.activation(out=sd[:, lo:hi], in_=mv[:, lo:hi, 1], func=ACT.Sqrt)
 
         nm_t = {}
         nmr_t = {}
@@ -238,14 +229,12 @@ def tile_rlstmcell_pa_t_kernel(tc, c_att, w1, w2, g1, g2, b1, b2, out):
             nc.scalar.mul(out=nm[:], in_=small_set(q)[0][:, 0:2, 0], mul=-1.0)
             nm_t[q] = nm
 
-        def s_eps(s):
+        def v_eps(s):
             lo, hi = span(s)
             if lo >= hi:
                 return
             sd = small_set(s)[1]
-            nc.scalar.activation(
-                out=sd[:, lo:hi], in_=sd[:, lo:hi], func=ACT.Identity, bias=epsc[:, 0:1]
-            )
+            nc.vector.tensor_scalar_add(out=sd[:, lo:hi], in0=sd[:, lo:hi], scalar1=EPS)
 
         def v_recip(s):
             lo, hi = span(s)
@@ -302,12 +291,13 @@ def tile_rlstmcell_pa_t_kernel(tc, c_att, w1, w2, g1, g2, b1, b2, out):
         def s_regroup(q, half):
             if not valid(q):
                 return
-            if half == 0:
+            if q not in hg_t:
                 hg_new = work3.tile([P, PAIR, 4], BF16, name="hg", align_bytes=64)
                 hg_t[q] = hg_new
             w = slice(half * P, (half + 1) * P)
             nc.scalar.copy(
-                out=hg_t[q][:, w, :], in_=ht_t[q][:, :, w].rearrange("p j w -> p w j")
+                out=hg_t[q][:, w, :].rearrange("p (c i) j -> p c j i", i=4),
+                in_=ht_t[q][:, :, w].rearrange("p j (c i) -> p c j i", i=4),
             )
 
         def v_quant_h(q):
@@ -364,50 +354,49 @@ def tile_rlstmcell_pa_t_kernel(tc, c_att, w1, w2, g1, g2, b1, b2, out):
                 return
             nc.sync.dma_start(out=o_pairs[q], in_=a_t[q][:].rearrange("p i d -> p (i d)"))
 
-        for t in range(-3, NPAIR + 6):
+        for t in range(-3, NPAIR + 5):
             v_recip(t)
             v_finish(t - 4, 0)
-            pe_zt(t - 1, 1)
-            v_bn1(t + 1, 0)
-            s_negmean(t)
-            pe_mx1(t + 1, 1)
-            s_hevac(t - 1, 0)
-            g_scale(t - 4, 1)
-            v_ag2(t - 3, 1)
             v_gain2(t - 3, 0)
             v_finish(t - 4, 1)
-            store(t - 6)
-            s_hevac(t - 1, 1)
-            load_x(t + 9)
-            s_sqrt2(t - 3)
-            s_hevac(t - 1, 3)
+            s_xevac(t + 2)
             g_negmean_r(t)
-            v_quant_h(t - 2)
-            s_hevac(t - 1, 2)
-            pe_xt(t + 3)
-            g_bias(t - 4, 1)
-            v_gain2(t - 3, 1)
+            g_scale(t - 4, 0)
+            v_bn1(t + 1, 0)
+            s_hevac(t - 1, 0)
             s_z1(t, 0)
+            pe_zt(t - 1, 1)
+            v_quant_h(t - 2)
+            g_bias(t - 5, 1)
+            v_gain2(t - 3, 1)
+            s_hevac(t - 1, 1)
+            s_z1(t, 1)
             pe_mx2(t - 2, 0)
             v_bn1(t + 1, 1)
-            s_z1(t, 1)
             pe_mx2(t - 2, 1)
-            s_regroup(t - 1, 0)
+            s_hevac(t - 1, 3)
             v_quant_x(t + 2)
             if t == -2:
                 prepare_late(0)
             if t == -1:
                 prepare_late(1)
-            g_scale(t - 4, 0)
+            pe_xt(t + 3)
+            s_hevac(t - 1, 2)
+            store(t - 5)
+            g_bias(t - 4, 0)
+            load_x(t + 10)
             v_ag1(t + 1, 0)
             v_ag1(t + 1, 1)
             v_bn2(t - 2, 0)
+            s_sqrt(t + 1)
             pe_mx1(t + 2, 0)
-            s_sqrt1(t + 1)
-            s_xevac(t + 3)
-            pe_zt(t, 0)
+            s_negmean(t + 1)
             v_bn2(t - 2, 1)
-            g_bias(t - 5, 0)
-            s_eps(t + 1)
             s_regroup(t - 1, 1)
+            pe_zt(t, 0)
+            g_scale(t - 4, 1)
+            pe_mx1(t + 2, 1)
+            v_eps(t + 1)
+            s_regroup(t - 1, 0)
             v_ag2(t - 2, 0)
+            v_ag2(t - 2, 1)

@@ -219,15 +219,7 @@ def tile_rlstmcell_pa_t_kernel(tc, c_att, w1, w2, g1, g2, b1, b2, out):
             mv, sd, rr = small_set(s)
             nc.scalar.activation(out=sd[:, lo:hi], in_=mv[:, lo:hi, 1], func=ACT.Sqrt)
 
-        nm_t = {}
         nmr_t = {}
-
-        def s_negmean(q):
-            if not valid(q):
-                return
-            nm = work3.tile([P, 2], F32, name="nm")
-            nc.scalar.mul(out=nm[:], in_=small_set(q)[0][:, 0:2, 0], mul=-1.0)
-            nm_t[q] = nm
 
         def v_eps(s):
             lo, hi = span(s)
@@ -243,12 +235,14 @@ def tile_rlstmcell_pa_t_kernel(tc, c_att, w1, w2, g1, g2, b1, b2, out):
             mv, sd, rr = small_set(s)
             nc.vector.reciprocal(out=rr[:, lo:hi], in_=sd[:, lo:hi])
 
-        def g_negmean_r(q):
+        def v_negmean_r(q):
             if not valid(q):
                 return
+            mv, sd, rr = small_set(q)
             nmr = work3.tile([P, 2], F32, name="nmr")
-            nc.gpsimd.tensor_tensor(
-                out=nmr[:], in0=nm_t[q][:], in1=small_set(q)[2][:, 0:2], op=ALU.mult
+            nc.vector.scalar_tensor_tensor(
+                out=nmr[:], in0=mv[:, 0:2, 0], scalar=-1.0, in1=rr[:, 0:2],
+                op0=ALU.mult, op1=ALU.mult,
             )
             nmr_t[q] = nmr
 
@@ -343,6 +337,15 @@ def tile_rlstmcell_pa_t_kernel(tc, c_att, w1, w2, g1, g2, b1, b2, out):
                 op0=ALU.mult, op1=ALU.add,
             )
 
+        def s_scale(q, i):
+            if not valid(q) or q in VECTOR_TAIL:
+                return
+            rr = small_set(q + LAG2)[2]
+            a = a_t[q]
+            nc.scalar.activation(
+                out=a[:, i, :], in_=a[:, i, :], func=ACT.Identity, scale=rr[:, 2 + i : 3 + i]
+            )
+
         def g_bias(q, i):
             if not valid(q) or q in VECTOR_TAIL:
                 return
@@ -357,46 +360,45 @@ def tile_rlstmcell_pa_t_kernel(tc, c_att, w1, w2, g1, g2, b1, b2, out):
         for t in range(-3, NPAIR + 5):
             v_recip(t)
             v_finish(t - 4, 0)
+            v_quant_h(t - 2)
+            pe_mx1(t + 1, 1)
+            s_hevac(t - 1, 0)
+            g_scale(t - 4, 0)
+            v_negmean_r(t)
             v_gain2(t - 3, 0)
             v_finish(t - 4, 1)
-            s_xevac(t + 2)
-            g_negmean_r(t)
-            g_scale(t - 4, 0)
-            v_bn1(t + 1, 0)
-            s_hevac(t - 1, 0)
-            s_z1(t, 0)
-            pe_zt(t - 1, 1)
-            v_quant_h(t - 2)
-            g_bias(t - 5, 1)
-            v_gain2(t - 3, 1)
             s_hevac(t - 1, 1)
-            s_z1(t, 1)
+            s_hevac(t - 1, 2)
+            v_gain2(t - 3, 1)
+            g_bias(t - 5, 0)
+            s_z1(t, 0)
             pe_mx2(t - 2, 0)
+            v_bn1(t + 1, 0)
+            pe_xt(t + 3)
+            s_hevac(t - 1, 3)
             v_bn1(t + 1, 1)
             pe_mx2(t - 2, 1)
-            s_hevac(t - 1, 3)
-            v_quant_x(t + 2)
-            if t == -2:
-                prepare_late(0)
-            if t == -1:
-                prepare_late(1)
-            pe_xt(t + 3)
-            s_hevac(t - 1, 2)
-            store(t - 5)
-            g_bias(t - 4, 0)
-            load_x(t + 10)
+            s_z1(t, 1)
+            g_bias(t - 5, 1)
             v_ag1(t + 1, 0)
-            v_ag1(t + 1, 1)
             v_bn2(t - 2, 0)
-            s_sqrt(t + 1)
-            pe_mx1(t + 2, 0)
-            s_negmean(t + 1)
-            v_bn2(t - 2, 1)
-            s_regroup(t - 1, 1)
-            pe_zt(t, 0)
-            g_scale(t - 4, 1)
-            pe_mx1(t + 2, 1)
-            v_eps(t + 1)
             s_regroup(t - 1, 0)
+            pe_zt(t, 0)
+            v_ag1(t + 1, 1)
+            s_xevac(t + 3)
+            v_bn2(t - 2, 1)
+            s_sqrt(t + 1)
             v_ag2(t - 2, 0)
+            store(t - 5)
+            s_regroup(t - 1, 1)
+            load_x(t + 10)
+            pe_zt(t, 1)
+            v_eps(t + 1)
+            v_quant_x(t + 3)
+            if t == -3:
+                prepare_late(0)
+            if t == -2:
+                prepare_late(1)
+            s_scale(t - 4, 1)
+            pe_mx1(t + 2, 0)
             v_ag2(t - 2, 1)

@@ -64,32 +64,33 @@ def tile_rlstmcell_pa_t_kernel(tc, c_att, w1, w2, g1, g2, b1, b2, out):
             nc.sync.dma_start(out=x_sb[:], in_=x_pairs[q])
             x_t[q] = x_sb
 
-        for q in range(2):
-            load_x(q)
-        gbr = const.tile([P, P], BF16, name="gbr")
-        nc.vector.memset(gbr[:], 0.0)
-        w1raw = const.tile([P, 4, D], BF16, name="w1raw")
-        nc.scalar.dma_start(
-            out=w1raw[:].rearrange("p (u e) n -> p u (e n)", u=2),
-            in_=w1.rearrange("(u p e) n -> p u (e n)", u=2, e=2),
-        )
-        nc.scalar.dma_start(out=gbr[0:4, :], in_=g1.rearrange("(j p) -> j p", p=P))
-        nc.scalar.dma_start(out=gbr[4:8, :], in_=b1.rearrange("(j p) -> j p", p=P))
-        w2raw = const.tile([P, 4, D], BF16, name="w2raw")
-        nc.scalar.dma_start(out=w2raw[:], in_=w2.rearrange("(t p) n -> p t n", p=P))
-        g2b = const.tile([P, D], BF16, name="g2b")
-        nc.scalar.dma_start(out=g2b[:], in_=g2.partition_broadcast(P))
-        b2b = const.tile([P, D], BF16, name="b2b")
-        nc.scalar.dma_start(out=b2b[:], in_=b2.partition_broadcast(P))
-        for q in range(2, FIRST_LOADS):
-            load_x(q)
-
         one = const.tile([P, 1], F32, name="one")
         nc.vector.memset(one[:], 1.0)
         nc.scalar.activation(out=one[:], in_=one[:], func=ACT.Sqrt)
-
+        gbr = const.tile([P, P], BF16, name="gbr")
+        nc.vector.memset(gbr[:], 0.0)
         ident = const.tile([P, P], F32, name="ident")
         make_identity(nc, ident[:])
+
+        w1raw = const.tile([P, 4, D], BF16, name="w1raw")
+        w2raw = const.tile([P, 4, D], BF16, name="w2raw")
+        g2b = const.tile([P, D], BF16, name="g2b")
+        b2b = const.tile([P, D], BF16, name="b2b")
+        nc.sync.dma_start(
+            out=w1raw[:].rearrange("p (u e) n -> p u (e n)", u=2),
+            in_=w1.rearrange("(u p e) n -> p u (e n)", u=2, e=2),
+        )
+        load_x(0)
+        nc.sync.dma_start(out=gbr[0:4, :], in_=g1.rearrange("(j p) -> j p", p=P))
+        nc.sync.dma_start(out=gbr[4:8, :], in_=b1.rearrange("(j p) -> j p", p=P))
+        load_x(1)
+        nc.sync.dma_start(out=w2raw[:], in_=w2.rearrange("(t p) n -> p t n", p=P))
+        load_x(2)
+        load_x(3)
+        nc.sync.dma_start(out=g2b[:], in_=g2.partition_broadcast(P))
+        nc.sync.dma_start(out=b2b[:], in_=b2.partition_broadcast(P))
+        for q in range(4, FIRST_LOADS):
+            load_x(q)
 
         w1g = const.tile([P, D, 4], BF16, name="w1g", align_bytes=64)
         w1q = const.tile([P, D], U32, name="w1q", align_bytes=64)
@@ -101,25 +102,42 @@ def tile_rlstmcell_pa_t_kernel(tc, c_att, w1, w2, g1, g2, b1, b2, out):
         b2f = const.tile([P, D], F32, name="b2f")
         gbf = const.tile([P, P], F32, name="gbf")
         gb1 = const.tile([P, 8], F32, name="gb1")
-        nc.vector.tensor_copy(out=w1g[:], in_=w1raw[:].rearrange("p t n -> p n t"))
-        nc.vector.quantize_mx(
-            out=w1q[:].bitcast(FP8X4), scales=w1s[:], in_=w1g[:].rearrange("p n t -> p (n t)")
-        )
 
-        def prepare_late(step):
-            if step == 0:
-                nc.vector.tensor_copy(out=gbf[:], in_=gbr[:])
-                gbt = ps_tp.tile([P, 2, PAIR], F32, name="gbt", tag="tp")
-                nc.tensor.transpose(gbt[:, 0, 0:P], gbf[:], ident[:])
-                nc.vector.tensor_copy(out=gb1[:], in_=gbt[:, 0, 0:8])
-                nc.vector.tensor_copy(out=w2g[:], in_=w2raw[:].rearrange("p t n -> p n t"))
-            else:
-                nc.vector.quantize_mx(
-                    out=w2q[:].bitcast(FP8X4), scales=w2s[:],
-                    in_=w2g[:].rearrange("p n t -> p (n t)"),
+        def v_prepare_w1():
+            nc.vector.tensor_copy(out=w1g[:], in_=w1raw[:].rearrange("p t n -> p n t"))
+            nc.vector.quantize_mx(
+                out=w1q[:].bitcast(FP8X4), scales=w1s[:],
+                in_=w1g[:].rearrange("p n t -> p (n t)"),
+            )
+
+        def s_group_w2(half):
+            w = slice(half * 2 * P, (half + 1) * 2 * P)
+            nc.scalar.copy(
+                out=w2g[:, w, :].rearrange("p (c i) j -> p c j i", i=4),
+                in_=w2raw[:, :, w].rearrange("p j (c i) -> p c j i", i=4),
+            )
+
+        def v_quant_w2():
+            nc.vector.quantize_mx(
+                out=w2q[:].bitcast(FP8X4), scales=w2s[:],
+                in_=w2g[:].rearrange("p n t -> p (n t)"),
+            )
+
+        def g_widen_gb1():
+            nc.gpsimd.tensor_scalar(
+                out=gbf[:], in0=gbr[:], scalar1=1.0, scalar2=0.0, op0=ALU.mult, op1=ALU.add
+            )
+
+        def pe_turn_gb1():
+            gbt = ps_tp.tile([P, 2, PAIR], F32, name="gbt", tag="tp")
+            nc.tensor.transpose(gbt[:, 0, 0:P], gbf[:], ident[:])
+            nc.vector.tensor_copy(out=gb1[:], in_=gbt[:, 0, 0:8])
+
+        def g_widen_gb2():
+            for wide, narrow in ((g2f, g2b), (b2f, b2b)):
+                nc.gpsimd.tensor_scalar(
+                    out=wide[:], in0=narrow[:], scalar1=1.0, scalar2=0.0, op0=ALU.mult, op1=ALU.add
                 )
-                nc.vector.tensor_copy(out=g2f[:], in_=g2b[:])
-                nc.vector.tensor_copy(out=b2f[:], in_=b2b[:])
 
         def pe_xt(q):
             if not valid(q):
@@ -357,6 +375,8 @@ def tile_rlstmcell_pa_t_kernel(tc, c_att, w1, w2, g1, g2, b1, b2, out):
                 return
             nc.sync.dma_start(out=o_pairs[q], in_=a_t[q][:].rearrange("p i d -> p (i d)"))
 
+        v_prepare_w1()
+        g_widen_gb1()
         for t in range(-3, NPAIR + 5):
             v_recip(t)
             v_finish(t - 4, 0)
@@ -395,10 +415,14 @@ def tile_rlstmcell_pa_t_kernel(tc, c_att, w1, w2, g1, g2, b1, b2, out):
             pe_zt(t, 1)
             v_eps(t + 1)
             v_quant_x(t + 3)
-            if t == -3:
-                prepare_late(0)
             if t == -2:
-                prepare_late(1)
+                s_group_w2(0)
+            if t == -1:
+                s_group_w2(1)
+                g_widen_gb2()
+                pe_turn_gb1()
+            if t == 0:
+                v_quant_w2()
             s_scale(t - 4, 1)
             pe_mx1(t + 2, 0)
             v_ag2(t - 2, 1)

@@ -198,10 +198,9 @@ def tile_rlstmcell_pa_t_kernel(tc, c_att, w1, w2, g1, g2, b1, b2, out):
 
         def small_set(s):
             if s not in set_t:
-                mv = work6.tile([P, 4, 2], F32, name="mv")
+                mvr = work6.tile([P, 4, 3], F32, name="mvr")
                 sd = work6.tile([P, 4], F32, name="sd")
-                rr = work6.tile([P, 4], F32, name="rr")
-                set_t[s] = (mv, sd, rr)
+                set_t[s] = (mvr, sd, mvr[:, :, 2])
             return set_t[s]
 
         def v_bn1(q, i):
@@ -215,7 +214,7 @@ def tile_rlstmcell_pa_t_kernel(tc, c_att, w1, w2, g1, g2, b1, b2, out):
         def v_ag1(q, i):
             if not valid(q):
                 return
-            nc.vector.bn_aggr(out=small_set(q)[0][:, i, :], in_=st1_t[q][:, i, :])
+            nc.vector.bn_aggr(out=small_set(q)[0][:, i, 0:2], in_=st1_t[q][:, i, :])
 
         def v_bn2(q, i):
             if not valid(q):
@@ -228,7 +227,7 @@ def tile_rlstmcell_pa_t_kernel(tc, c_att, w1, w2, g1, g2, b1, b2, out):
         def v_ag2(q, i):
             if not valid(q):
                 return
-            nc.vector.bn_aggr(out=small_set(q + LAG2)[0][:, 2 + i, :], in_=st2_t[q][:, i, :])
+            nc.vector.bn_aggr(out=small_set(q + LAG2)[0][:, 2 + i, 0:2], in_=st2_t[q][:, i, :])
 
         def s_sqrt(s):
             lo, hi = span(s)
@@ -256,11 +255,11 @@ def tile_rlstmcell_pa_t_kernel(tc, c_att, w1, w2, g1, g2, b1, b2, out):
         def v_negmean_r(q):
             if not valid(q):
                 return
-            mv, sd, rr = small_set(q)
+            mvr = small_set(q)[0]
             nmr = work3.tile([P, 2], F32, name="nmr")
-            nc.vector.scalar_tensor_tensor(
-                out=nmr[:], in0=mv[:, 0:2, 0], scalar=-1.0, in1=rr[:, 0:2],
-                op0=ALU.mult, op1=ALU.mult,
+            nc.vector.tensor_reduce(
+                out=nmr[:], in_=mvr[:, 0:2, 0:3:2], axis=mybir.AxisListType.X, op=ALU.mult,
+                negate=True,
             )
             nmr_t[q] = nmr
 

@@ -20,7 +20,6 @@ EPS = 1e-9
 FLOPS = 2 * 2 * TOKENS * D * D
 LAG2 = 4
 FIRST_LOADS = 7
-VECTOR_TAIL = (30, 31)
 
 
 def tile_rlstmcell_pa_t_kernel(tc, c_att, w1, w2, g1, g2, b1, b2, out):
@@ -67,6 +66,8 @@ def tile_rlstmcell_pa_t_kernel(tc, c_att, w1, w2, g1, g2, b1, b2, out):
         one = const.tile([P, 1], F32, name="one")
         nc.vector.memset(one[:], 1.0)
         nc.scalar.activation(out=one[:], in_=one[:], func=ACT.Sqrt)
+        eps = const.tile([P, 1], F32, name="eps")
+        nc.vector.memset(eps[:], EPS)
         gbr = const.tile([P, P], BF16, name="gbr")
         nc.vector.memset(gbr[:], 0.0)
         ident = const.tile([P, P], F32, name="ident")
@@ -99,7 +100,7 @@ def tile_rlstmcell_pa_t_kernel(tc, c_att, w1, w2, g1, g2, b1, b2, out):
         w2q = const.tile([P, D], U32, name="w2q", align_bytes=64)
         w2s = const.tile([P, D], U8, name="w2s", align_bytes=64)
         g2f = const.tile([P, D], F32, name="g2f")
-        b2f = const.tile([P, D], F32, name="b2f")
+        b2f = const.tile([P, 2, D], F32, name="b2f")
         gbf = const.tile([P, P], F32, name="gbf")
         gb1 = const.tile([P, 8], F32, name="gb1")
 
@@ -134,9 +135,9 @@ def tile_rlstmcell_pa_t_kernel(tc, c_att, w1, w2, g1, g2, b1, b2, out):
             nc.vector.tensor_copy(out=gb1[:], in_=gbt[:, 0, 0:8])
 
         def g_widen_gb2():
-            for wide, narrow in ((g2f, g2b), (b2f, b2b)):
+            for wide, narrow in ((g2f[:], g2b), (b2f[:, 0, :], b2b), (b2f[:, 1, :], b2b)):
                 nc.gpsimd.tensor_scalar(
-                    out=wide[:], in0=narrow[:], scalar1=1.0, scalar2=0.0, op0=ALU.mult, op1=ALU.add
+                    out=wide, in0=narrow[:], scalar1=1.0, scalar2=0.0, op0=ALU.mult, op1=ALU.add
                 )
 
         def pe_xt(q):
@@ -191,6 +192,9 @@ def tile_rlstmcell_pa_t_kernel(tc, c_att, w1, w2, g1, g2, b1, b2, out):
         def pe_mx2(q, i):
             pe_mx(q, i, hq_t, w2q, w2s, ps_y2, "y2", y2_t)
 
+        def pe_mx2_last(q, i):
+            pe_mx(q, i, hq_t, w2q, w2s, ps_y1, "y1", y2_t)
+
         def span(s):
             lo = 0 if valid(s) else 2
             hi = 4 if valid(s - LAG2) else 2
@@ -244,6 +248,13 @@ def tile_rlstmcell_pa_t_kernel(tc, c_att, w1, w2, g1, g2, b1, b2, out):
                 return
             sd = small_set(s)[1]
             nc.vector.tensor_scalar_add(out=sd[:, lo:hi], in0=sd[:, lo:hi], scalar1=EPS)
+
+        def s_eps(s):
+            lo, hi = span(s)
+            sd = small_set(s)[1]
+            nc.scalar.activation(
+                out=sd[:, lo:hi], in_=sd[:, lo:hi], func=ACT.Identity, bias=eps[:, 0:1]
+            )
 
         def v_recip(s):
             lo, hi = span(s)
@@ -335,17 +346,17 @@ def tile_rlstmcell_pa_t_kernel(tc, c_att, w1, w2, g1, g2, b1, b2, out):
             )
 
         def v_finish(q, i):
-            if not valid(q) or q not in VECTOR_TAIL:
+            if not valid(q):
                 return
             rr = small_set(q + LAG2)[2]
             a = a_t[q]
             nc.vector.scalar_tensor_tensor(
-                out=a[:, i, :], in0=a[:, i, :], scalar=rr[:, 2 + i : 3 + i], in1=b2f[:],
+                out=a[:, i, :], in0=a[:, i, :], scalar=rr[:, 2 + i : 3 + i], in1=b2f[:, i, :],
                 op0=ALU.mult, op1=ALU.add,
             )
 
         def g_scale(q, i):
-            if not valid(q) or q in VECTOR_TAIL:
+            if not valid(q):
                 return
             rr = small_set(q + LAG2)[2]
             a = a_t[q]
@@ -355,7 +366,7 @@ def tile_rlstmcell_pa_t_kernel(tc, c_att, w1, w2, g1, g2, b1, b2, out):
             )
 
         def s_scale(q, i):
-            if not valid(q) or q in VECTOR_TAIL:
+            if not valid(q):
                 return
             rr = small_set(q + LAG2)[2]
             a = a_t[q]
@@ -363,11 +374,16 @@ def tile_rlstmcell_pa_t_kernel(tc, c_att, w1, w2, g1, g2, b1, b2, out):
                 out=a[:, i, :], in_=a[:, i, :], func=ACT.Identity, scale=rr[:, 2 + i : 3 + i]
             )
 
-        def g_bias(q, i):
-            if not valid(q) or q in VECTOR_TAIL:
+        def g_bias(q):
+            if not valid(q):
                 return
             a = a_t[q]
-            nc.gpsimd.tensor_tensor(out=a[:, i, :], in0=a[:, i, :], in1=b2f[:], op=ALU.add)
+            nc.gpsimd.tensor_tensor(out=a[:], in0=a[:], in1=b2f[:], op=ALU.add)
+
+        def store_tile(q, i):
+            nc.sync.dma_start(
+                out=o_pairs[q][:, i * D : (i + 1) * D], in_=a_t[q][:, i, :]
+            )
 
         def store(q):
             if not valid(q):
@@ -376,20 +392,17 @@ def tile_rlstmcell_pa_t_kernel(tc, c_att, w1, w2, g1, g2, b1, b2, out):
 
         v_prepare_w1()
         g_widen_gb1()
-        for t in range(-3, NPAIR + 5):
+        for t in range(-3, NPAIR):
             v_recip(t)
-            v_finish(t - 4, 0)
             v_quant_h(t - 2)
             pe_mx1(t + 1, 1)
             s_hevac(t - 1, 0)
             g_scale(t - 4, 0)
             v_negmean_r(t)
             v_gain2(t - 3, 0)
-            v_finish(t - 4, 1)
             s_hevac(t - 1, 1)
             s_hevac(t - 1, 2)
             v_gain2(t - 3, 1)
-            g_bias(t - 5, 0)
             s_z1(t, 0)
             pe_mx2(t - 2, 0)
             v_bn1(t + 1, 0)
@@ -398,7 +411,7 @@ def tile_rlstmcell_pa_t_kernel(tc, c_att, w1, w2, g1, g2, b1, b2, out):
             v_bn1(t + 1, 1)
             pe_mx2(t - 2, 1)
             s_z1(t, 1)
-            g_bias(t - 5, 1)
+            g_bias(t - 5)
             v_ag1(t + 1, 0)
             v_bn2(t - 2, 0)
             s_regroup(t - 1, 0)
@@ -425,3 +438,56 @@ def tile_rlstmcell_pa_t_kernel(tc, c_att, w1, w2, g1, g2, b1, b2, out):
             s_scale(t - 4, 1)
             pe_mx1(t + 2, 0)
             v_ag2(t - 2, 1)
+
+        v_recip(32)
+        v_quant_h(30)
+        s_hevac(31, 0)
+        s_sqrt(33)
+        s_hevac(31, 1)
+        s_hevac(31, 2)
+        s_eps(33)
+        s_hevac(31, 3)
+        v_gain2(29, 0)
+        pe_mx2_last(30, 0)
+        pe_mx2_last(30, 1)
+        g_bias(27)
+        store(27)
+        v_gain2(29, 1)
+        s_scale(28, 0)
+        s_regroup(31, 0)
+        s_regroup(31, 1)
+        v_bn2(30, 0)
+        v_recip(33)
+        v_bn2(30, 1)
+        s_scale(28, 1)
+        v_ag2(30, 0)
+        v_ag2(30, 1)
+        v_finish(29, 0)
+        v_quant_h(31)
+        s_sqrt(34)
+        pe_mx2_last(31, 0)
+        pe_mx2_last(31, 1)
+        v_finish(29, 1)
+        s_eps(34)
+        store(29)
+        g_bias(28)
+        store(28)
+        v_gain2(30, 0)
+        v_gain2(30, 1)
+        v_bn2(31, 0)
+        v_recip(34)
+        v_bn2(31, 1)
+        v_ag2(31, 0)
+        v_finish(30, 0)
+        v_ag2(31, 1)
+        s_sqrt(35)
+        v_finish(30, 1)
+        store(30)
+        s_eps(35)
+        v_gain2(31, 0)
+        v_gain2(31, 1)
+        v_recip(35)
+        v_finish(31, 0)
+        store_tile(31, 0)
+        v_finish(31, 1)
+        store_tile(31, 1)

@@ -30,8 +30,8 @@ def tile_rlstmcell_pa_t_kernel(tc, c_att, w1, w2, g1, g2, b1, b2, out):
     with ExitStack() as ctx:
         ctx.enter_context(tc.manual_schedule())
         const = ctx.enter_context(tc.tile_pool(name="const", bufs=1))
-        xin = ctx.enter_context(tc.tile_pool(name="xin", bufs=FIRST_LOADS + 3))
-        work3 = ctx.enter_context(tc.tile_pool(name="work3", bufs=3))
+        xin = ctx.enter_context(tc.tile_pool(name="xin", bufs=FIRST_LOADS + 6))
+        work3 = ctx.enter_context(tc.tile_pool(name="work3", bufs=4))
         work6 = ctx.enter_context(tc.tile_pool(name="work6", bufs=6))
         ps_tp = ctx.enter_context(tc.psum_pool(name="ps_tp", bufs=2))
         ps_y1 = ctx.enter_context(tc.psum_pool(name="ps_y1", bufs=4))
@@ -111,9 +111,9 @@ def tile_rlstmcell_pa_t_kernel(tc, c_att, w1, w2, g1, g2, b1, b2, out):
                 in_=w1g[:].rearrange("p n t -> p (n t)"),
             )
 
-        def s_group_w2(half):
+        def v_group_w2(half):
             w = slice(half * 2 * P, (half + 1) * 2 * P)
-            nc.scalar.copy(
+            nc.vector.tensor_copy(
                 out=w2g[:, w, :].rearrange("p (c i) j -> p c j i", i=4),
                 in_=w2raw[:, :, w].rearrange("p j (c i) -> p c j i", i=4),
             )
@@ -140,16 +140,24 @@ def tile_rlstmcell_pa_t_kernel(tc, c_att, w1, w2, g1, g2, b1, b2, out):
                     out=wide, in0=narrow[:], scalar1=1.0, scalar2=0.0, op0=ALU.mult, op1=ALU.add
                 )
 
-        def pe_xt(q):
+        def pe_xt(q, pool=ps_tp, tag="tp"):
             if not valid(q):
                 return
-            xt = ps_tp.tile([P, 2, 2, P], F32, name="xt", tag="tp")
+            xt = pool.tile([P, 2, 2, P], F32, name="xt", tag=tag)
             x32 = x_t[q][:].bitcast(F32)
             for i in range(2):
                 for u in range(2):
                     c0 = 256 * i + 128 * u
                     nc.tensor.transpose(xt[:, i, u, :], x32[:, c0 : c0 + P], ident[:])
             xt_t[q] = xt
+
+        def v_xevac(q):
+            xg = work3.tile([P, 4 * PAIR], BF16, name="xg", align_bytes=64)
+            nc.vector.tensor_copy(
+                out=xg[:].bitcast(F32).rearrange("p (i w u) -> p i w u", i=2, u=2),
+                in_=xt_t[q][:].rearrange("p i u w -> p i w u"),
+            )
+            xg_t[q] = xg
 
         def s_xevac(q):
             if not valid(q):
@@ -278,12 +286,23 @@ def tile_rlstmcell_pa_t_kernel(tc, c_att, w1, w2, g1, g2, b1, b2, out):
             if not valid(q):
                 return
             rr = small_set(q)[2]
-            if i == 0:
+            if q not in z_t:
                 z_new = work3.tile([P, 2, D], F32, name="z")
                 z_t[q] = z_new
             nc.scalar.activation(
                 out=z_t[q][:, i, :], in_=y1_t[(q, i)][:], func=ACT.Identity,
                 scale=rr[:, i : i + 1], bias=nmr_t[q][:, i : i + 1],
+            )
+
+        def v_z1(q, i):
+            mvr = small_set(q)[0]
+            if q not in z_t:
+                z_new = work3.tile([P, 2, D], F32, name="z")
+                z_t[q] = z_new
+            nc.vector.tensor_scalar(
+                out=z_t[q][:, i, :], in0=y1_t[(q, i)][:],
+                scalar1=mvr[:, i, 0:1], scalar2=mvr[:, i, 2:3],
+                op0=ALU.subtract, op1=ALU.mult,
             )
 
         def pe_zt(q, h):
@@ -310,16 +329,15 @@ def tile_rlstmcell_pa_t_kernel(tc, c_att, w1, w2, g1, g2, b1, b2, out):
                 scale=gb1[:, j : j + 1], bias=gb1[:, 4 + j : 5 + j],
             )
 
-        def s_regroup(q, half):
+        def s_regroup(q):
             if not valid(q):
                 return
             if q not in hg_t:
                 hg_new = work3.tile([P, PAIR, 4], BF16, name="hg", align_bytes=64)
                 hg_t[q] = hg_new
-            w = slice(half * P, (half + 1) * P)
             nc.scalar.copy(
-                out=hg_t[q][:, w, :].rearrange("p (c i) j -> p c j i", i=4),
-                in_=ht_t[q][:, :, w].rearrange("p j (c i) -> p c j i", i=4),
+                out=hg_t[q][:].rearrange("p (c i) j -> p c j i", i=4),
+                in_=ht_t[q][:].rearrange("p j (c i) -> p c j i", i=4),
             )
 
         def v_quant_h(q):
@@ -392,55 +410,113 @@ def tile_rlstmcell_pa_t_kernel(tc, c_att, w1, w2, g1, g2, b1, b2, out):
 
         v_prepare_w1()
         g_widen_gb1()
-        for t in range(-3, NPAIR):
-            v_recip(t)
-            v_quant_h(t - 2)
+        for q in range(FIRST_LOADS, 13):
+            load_x(q)
+        pe_xt(0)
+        pe_xt(1)
+        s_xevac(0)
+        s_xevac(1)
+        v_quant_x(0)
+        v_quant_x(1)
+        pe_mx1(0, 0)
+        pe_mx1(0, 1)
+        pe_xt(2)
+        pe_mx1(1, 0)
+        pe_mx1(1, 1)
+        s_xevac(2)
+        v_bn1(0, 0)
+        v_bn1(0, 1)
+        v_ag1(0, 0)
+        v_ag1(0, 1)
+        pe_turn_gb1()
+        pe_xt(3)
+        pe_xt(4, ps_y2, "y2")
+        pe_xt(5, ps_y2, "y2")
+        s_sqrt(0)
+        s_xevac(3)
+        s_xevac(4)
+        v_bn1(1, 0)
+        v_eps(0)
+        v_quant_x(2)
+        v_recip(0)
+        v_ag1(1, 0)
+        v_negmean_r(0)
+        s_z1(0, 0)
+        v_bn1(1, 1)
+        v_ag1(1, 1)
+        s_z1(0, 1)
+        s_sqrt(1)
+        s_xevac(5)
+        pe_zt(0, 0)
+        pe_zt(0, 1)
+        v_quant_x(3)
+        v_group_w2(0)
+        v_eps(1)
+        g_widen_gb2()
+        v_group_w2(1)
+        v_recip(1)
+        pe_mx1(2, 0)
+        pe_mx1(2, 1)
+        s_hevac(0, 0)
+        v_z1(1, 0)
+        s_hevac(0, 1)
+        v_z1(1, 1)
+        s_hevac(0, 2)
+        s_hevac(0, 3)
+        v_bn1(2, 0)
+        pe_zt(1, 0)
+        pe_zt(1, 1)
+        v_bn1(2, 1)
+        v_ag1(2, 0)
+        v_ag1(2, 1)
+        s_regroup(0)
+        s_sqrt(2)
+        v_quant_w2()
+        pe_mx1(3, 0)
+        for t in range(2, NPAIR):
+            v_quant_x(t + 2)
             pe_mx1(t + 1, 1)
+            v_ag2(t - 3, 1)
+            v_eps(t)
+            v_quant_h(t - 2)
+            v_recip(t)
             s_hevac(t - 1, 0)
             g_scale(t - 4, 0)
-            v_negmean_r(t)
-            v_gain2(t - 3, 0)
+            if t < 4:
+                v_negmean_r(t)
+            v_bn1(t + 1, 0)
             s_hevac(t - 1, 1)
             s_hevac(t - 1, 2)
-            v_gain2(t - 3, 1)
+            if t >= 4:
+                v_negmean_r(t)
+            v_gain2(t - 3, 0)
             s_z1(t, 0)
+            v_gain2(t - 3, 1)
+            pe_xt(t + 4)
             pe_mx2(t - 2, 0)
-            v_bn1(t + 1, 0)
-            pe_xt(t + 3)
+            pe_mx2(t - 2, 1)
             s_hevac(t - 1, 3)
             v_bn1(t + 1, 1)
-            pe_mx2(t - 2, 1)
             s_z1(t, 1)
             g_bias(t - 5)
+            store(t - 5)
             v_ag1(t + 1, 0)
             v_bn2(t - 2, 0)
-            s_regroup(t - 1, 0)
-            pe_zt(t, 0)
             v_ag1(t + 1, 1)
-            s_xevac(t + 3)
+            pe_zt(t, 0)
+            s_regroup(t - 1)
             v_bn2(t - 2, 1)
             s_sqrt(t + 1)
+            s_xevac(t + 4)
             v_ag2(t - 2, 0)
-            store(t - 5)
-            s_regroup(t - 1, 1)
-            load_x(t + 10)
-            pe_zt(t, 1)
-            v_eps(t + 1)
-            v_quant_x(t + 3)
-            if t == -2:
-                s_group_w2(0)
-            if t == -1:
-                s_group_w2(1)
-                g_widen_gb2()
-                pe_turn_gb1()
-            if t == 0:
-                v_quant_w2()
-            s_scale(t - 4, 1)
+            load_x(t + 11)
             pe_mx1(t + 2, 0)
-            v_ag2(t - 2, 1)
+            pe_zt(t, 1)
+            (g_scale if t % 4 == 0 else s_scale)(t - 4, 1)
 
-        v_recip(32)
+        v_ag2(29, 1)
         v_quant_h(30)
+        v_eps(32)
         s_hevac(31, 0)
         s_sqrt(33)
         s_hevac(31, 1)
@@ -448,14 +524,14 @@ def tile_rlstmcell_pa_t_kernel(tc, c_att, w1, w2, g1, g2, b1, b2, out):
         s_eps(33)
         s_hevac(31, 3)
         v_gain2(29, 0)
+        v_recip(32)
         pe_mx2_last(30, 0)
         pe_mx2_last(30, 1)
         g_bias(27)
         store(27)
         v_gain2(29, 1)
         s_scale(28, 0)
-        s_regroup(31, 0)
-        s_regroup(31, 1)
+        s_regroup(31)
         v_bn2(30, 0)
         v_recip(33)
         v_bn2(30, 1)

@@ -512,7 +512,7 @@ def tile_rlstmcell_pa_t_kernel(tc, c_att, w1, w2, g1, g2, b1, b2, out):
             load_x(t + 11)
             pe_mx1(t + 2, 0)
             pe_zt(t, 1)
-            (g_scale if t % 4 == 0 else s_scale)(t - 4, 1)
+            s_scale(t - 4, 1)
 
         v_ag2(29, 1)
         v_quant_h(30)

@@ -88,8 +88,6 @@ def tile_rlstmcell_pa_t_kernel(tc, c_att, w1, w2, g1, g2, b1, b2, out):
         nc.sync.dma_start(out=w2raw[:], in_=w2.rearrange("(t p) n -> p t n", p=P))
         load_x(2)
         load_x(3)
-        nc.sync.dma_start(out=g2b[:], in_=g2.partition_broadcast(P))
-        nc.sync.dma_start(out=b2b[:], in_=b2.partition_broadcast(P))
         for q in range(4, FIRST_LOADS):
             load_x(q)
 
@@ -410,7 +408,11 @@ def tile_rlstmcell_pa_t_kernel(tc, c_att, w1, w2, g1, g2, b1, b2, out):
 
         v_prepare_w1()
         g_widen_gb1()
-        for q in range(FIRST_LOADS, 13):
+        for q in range(FIRST_LOADS, 9):
+            load_x(q)
+        nc.sync.dma_start(out=g2b[:], in_=g2.partition_broadcast(P))
+        nc.sync.dma_start(out=b2b[:], in_=b2.partition_broadcast(P))
+        for q in range(9, 13):
             load_x(q)
         pe_xt(0)
         pe_xt(1)

@@ -138,6 +138,11 @@ def tile_rlstmcell_pa_t_kernel(tc, c_att, w1, w2, g1, g2, b1, b2, out):
                     out=wide, in0=narrow[:], scalar1=1.0, scalar2=0.0, op0=ALU.mult, op1=ALU.add
                 )
 
+        def pe_warm(bank):
+            nc.tensor.matmul(
+                out=bank[:, 0:P], lhsT=ident[:], rhs=ident[:], start=True, stop=True
+            )
+
         def pe_xt(q, pool=ps_tp, tag="tp"):
             if not valid(q):
                 return
@@ -179,7 +184,7 @@ def tile_rlstmcell_pa_t_kernel(tc, c_att, w1, w2, g1, g2, b1, b2, out):
             if not valid(q):
                 return
             codes, scales = src[q]
-            acc = pool.tile([P, D], F32, name=nm)
+            acc = dst[(q, i)] if (q, i) in dst else pool.tile([P, D], F32, name=nm)
             cols = slice(i * P, (i + 1) * P)
             nc.tensor.matmul_mx(
                 out=acc[:],
@@ -191,6 +196,14 @@ def tile_rlstmcell_pa_t_kernel(tc, c_att, w1, w2, g1, g2, b1, b2, out):
                 stop=True,
             )
             dst[(q, i)] = acc
+
+        def pe_warm_y1(q, i):
+            if not valid(q):
+                return
+            if (q, i) not in y1_t:
+                acc = ps_y1.tile([P, D], F32, name="y1")
+                y1_t[(q, i)] = acc
+            pe_warm(y1_t[(q, i)])
 
         def pe_mx1(q, i):
             pe_mx(q, i, xq_t, w1q, w1s, ps_y1, "y1", y1_t)
@@ -477,6 +490,7 @@ def tile_rlstmcell_pa_t_kernel(tc, c_att, w1, w2, g1, g2, b1, b2, out):
         pe_mx1(3, 0)
         for t in range(2, NPAIR):
             v_quant_x(t + 2)
+            pe_warm_y1(t + 1, 1)
             pe_mx1(t + 1, 1)
             v_ag2(t - 3, 1)
             v_eps(t)
@@ -497,6 +511,7 @@ def tile_rlstmcell_pa_t_kernel(tc, c_att, w1, w2, g1, g2, b1, b2, out):
             pe_xt(t + 4)
             pe_mx2(t - 2, 0)
             pe_mx2(t - 2, 1)
+            pe_warm_y1(t + 2, 0)
             s_hevac(t - 1, 3)
             v_bn1(t + 1, 1)
             s_z1(t, 1)
@@ -513,6 +528,7 @@ def tile_rlstmcell_pa_t_kernel(tc, c_att, w1, w2, g1, g2, b1, b2, out):
             v_ag2(t - 2, 0)
             load_x(t + 11)
             pe_mx1(t + 2, 0)
+            pe_warm_y1(t + 2, 1)
             pe_zt(t, 1)
             s_scale(t - 4, 1)
 

@@ -138,10 +138,12 @@ def tile_rlstmcell_pa_t_kernel(tc, c_att, w1, w2, g1, g2, b1, b2, out):
                     out=wide, in0=narrow[:], scalar1=1.0, scalar2=0.0, op0=ALU.mult, op1=ALU.add
                 )
 
-        def pe_warm(bank):
-            nc.tensor.matmul(
-                out=bank[:, 0:P], lhsT=ident[:], rhs=ident[:], start=True, stop=True
-            )
+        def pe_warm(bank, times=1):
+            for k in range(times):
+                nc.tensor.matmul(
+                    out=bank[:, (k % 4) * P : (k % 4 + 1) * P],
+                    lhsT=ident[:], rhs=ident[:], start=True, stop=True,
+                )
 
         def pe_xt(q, pool=ps_tp, tag="tp"):
             if not valid(q):
@@ -197,13 +199,14 @@ def tile_rlstmcell_pa_t_kernel(tc, c_att, w1, w2, g1, g2, b1, b2, out):
             )
             dst[(q, i)] = acc
 
-        def pe_warm_y1(q, i):
-            if not valid(q):
-                return
-            if (q, i) not in y1_t:
+        def pe_warm_y(dst, q, i, times=1):
+            if (q, i) not in dst:
                 acc = ps_y1.tile([P, D], F32, name="y1")
-                y1_t[(q, i)] = acc
-            pe_warm(y1_t[(q, i)])
+                dst[(q, i)] = acc
+            pe_warm(dst[(q, i)], times)
+
+        def pe_warm_y1(q, i, times=1):
+            pe_warm_y(y1_t, q, i, times)
 
         def pe_mx1(q, i):
             pe_mx(q, i, xq_t, w1q, w1s, ps_y1, "y1", y1_t)
@@ -316,18 +319,23 @@ def tile_rlstmcell_pa_t_kernel(tc, c_att, w1, w2, g1, g2, b1, b2, out):
                 op0=ALU.subtract, op1=ALU.mult,
             )
 
+        def new_zt(q, h):
+            zt = ps_tp.tile([P, 2, PAIR], F32, name="zt", tag="tp")
+            zt_t[(q, h)] = zt
+
         def pe_zt(q, h):
             if not valid(q):
                 return
             z = z_t[q]
-            zt = ps_tp.tile([P, 2, PAIR], F32, name="zt", tag="tp")
+            if (q, h) not in zt_t:
+                new_zt(q, h)
+            zt = zt_t[(q, h)]
             for jj in range(2):
                 j = 2 * h + jj
                 for i in range(2):
                     nc.tensor.transpose(
                         zt[:, jj, i * P : (i + 1) * P], z[:, i, j * P : (j + 1) * P], ident[:]
                     )
-            zt_t[(q, h)] = zt
 
         def s_hevac(q, j):
             if not valid(q):
@@ -427,8 +435,10 @@ def tile_rlstmcell_pa_t_kernel(tc, c_att, w1, w2, g1, g2, b1, b2, out):
         nc.sync.dma_start(out=b2b[:], in_=b2.partition_broadcast(P))
         for q in range(9, 13):
             load_x(q)
+        pe_warm_y1(0, 0, 4)
         pe_xt(0)
         pe_xt(1)
+        pe_warm_y1(0, 1, 2)
         s_xevac(0)
         s_xevac(1)
         v_quant_x(0)
@@ -447,6 +457,8 @@ def tile_rlstmcell_pa_t_kernel(tc, c_att, w1, w2, g1, g2, b1, b2, out):
         pe_xt(3)
         pe_xt(4, ps_y2, "y2")
         pe_xt(5, ps_y2, "y2")
+        new_zt(0, 0)
+        pe_warm(zt_t[(0, 0)][:].rearrange("p j w -> p (j w)"), 4)
         s_sqrt(0)
         s_xevac(3)
         s_xevac(4)
@@ -508,9 +520,9 @@ def tile_rlstmcell_pa_t_kernel(tc, c_att, w1, w2, g1, g2, b1, b2, out):
             v_gain2(t - 3, 0)
             s_z1(t, 0)
             v_gain2(t - 3, 1)
-            pe_xt(t + 4)
             pe_mx2(t - 2, 0)
             pe_mx2(t - 2, 1)
+            pe_xt(t + 4)
             pe_warm_y1(t + 2, 0)
             s_hevac(t - 1, 3)
             v_bn1(t + 1, 1)
@@ -545,6 +557,7 @@ def tile_rlstmcell_pa_t_kernel(tc, c_att, w1, w2, g1, g2, b1, b2, out):
         v_recip(32)
         pe_mx2_last(30, 0)
         pe_mx2_last(30, 1)
+        pe_warm_y(y2_t, 31, 0, 4)
         g_bias(27)
         store(27)
         v_gain2(29, 1)

@@ -97,7 +97,6 @@ def tile_rlstmcell_pa_t_kernel(tc, c_att, w1, w2, g1, g2, b1, b2, out):
         w2g = const.tile([P, D, 4], BF16, name="w2g", align_bytes=64)
         w2q = const.tile([P, D], U32, name="w2q", align_bytes=64)
         w2s = const.tile([P, D], U8, name="w2s", align_bytes=64)
-        g2f = const.tile([P, D], F32, name="g2f")
         b2f = const.tile([P, 2, D], F32, name="b2f")
         gbf = const.tile([P, P], F32, name="gbf")
         gb1 = const.tile([P, 8], F32, name="gb1")
@@ -132,10 +131,10 @@ def tile_rlstmcell_pa_t_kernel(tc, c_att, w1, w2, g1, g2, b1, b2, out):
             nc.tensor.transpose(gbt[:, 0, 0:P], gbf[:], ident[:])
             nc.vector.tensor_copy(out=gb1[:], in_=gbt[:, 0, 0:8])
 
-        def g_widen_gb2():
-            for wide, narrow in ((g2f[:], g2b), (b2f[:, 0, :], b2b), (b2f[:, 1, :], b2b)):
+        def g_widen_b2():
+            for i in range(2):
                 nc.gpsimd.tensor_scalar(
-                    out=wide, in0=narrow[:], scalar1=1.0, scalar2=0.0, op0=ALU.mult, op1=ALU.add
+                    out=b2f[:, i, :], in0=b2b[:], scalar1=1.0, scalar2=0.0, op0=ALU.mult, op1=ALU.add
                 )
 
         def pe_warm(bank, times=1):
@@ -163,6 +162,16 @@ def tile_rlstmcell_pa_t_kernel(tc, c_att, w1, w2, g1, g2, b1, b2, out):
                 in_=xt_t[q][:].rearrange("p i u w -> p i w u"),
             )
             xg_t[q] = xg
+
+        def x_part(copy, q, cols):
+            if not valid(q):
+                return
+            if q not in xg_t:
+                xg = work3.tile([P, 4 * PAIR], BF16, name="xg", align_bytes=64)
+                xg_t[q] = xg
+            xg32 = xg_t[q][:].bitcast(F32).rearrange("p (i w u) -> p i w u", i=2, u=2)
+            xt = xt_t[q][:].rearrange("p i u w -> p i w u")
+            copy(out=xg32[:, :, cols, :], in_=xt[:, :, cols, :])
 
         def s_xevac(q):
             if not valid(q):
@@ -378,7 +387,7 @@ def tile_rlstmcell_pa_t_kernel(tc, c_att, w1, w2, g1, g2, b1, b2, out):
                 a_t[q] = a_new
             mv = small_set(q + LAG2)[0]
             nc.vector.scalar_tensor_tensor(
-                out=a_t[q][:, i, :], in0=y2_t[(q, i)][:], scalar=mv[:, 2 + i, 0:1], in1=g2f[:],
+                out=a_t[q][:, i, :], in0=y2_t[(q, i)][:], scalar=mv[:, 2 + i, 0:1], in1=g2b[:],
                 op0=ALU.subtract, op1=ALU.mult,
             )
 
@@ -417,6 +426,12 @@ def tile_rlstmcell_pa_t_kernel(tc, c_att, w1, w2, g1, g2, b1, b2, out):
             a = a_t[q]
             nc.gpsimd.tensor_tensor(out=a[:], in0=a[:], in1=b2f[:], op=ALU.add)
 
+        def g_bias_tile(q, i):
+            a = a_t[q]
+            nc.gpsimd.tensor_tensor(
+                out=a[:, i, :], in0=a[:, i, :], in1=b2f[:, i, :], op=ALU.add
+            )
+
         def store_tile(q, i):
             nc.sync.dma_start(
                 out=o_pairs[q][:, i * D : (i + 1) * D], in_=a_t[q][:, i, :]
@@ -432,7 +447,6 @@ def tile_rlstmcell_pa_t_kernel(tc, c_att, w1, w2, g1, g2, b1, b2, out):
         for q in range(FIRST_LOADS, 9):
             load_x(q)
         nc.sync.dma_start(out=g2b[:], in_=g2.partition_broadcast(P))
-        nc.sync.dma_start(out=b2b[:], in_=b2.partition_broadcast(P))
         for q in range(9, 13):
             load_x(q)
         pe_warm_y1(0, 0, 4)
@@ -469,26 +483,25 @@ def tile_rlstmcell_pa_t_kernel(tc, c_att, w1, w2, g1, g2, b1, b2, out):
         v_ag1(1, 0)
         v_negmean_r(0)
         s_z1(0, 0)
-        v_bn1(1, 1)
-        v_ag1(1, 1)
-        s_z1(0, 1)
-        s_sqrt(1)
+        v_z1(0, 1)
         s_xevac(5)
         pe_zt(0, 0)
         pe_zt(0, 1)
+        v_bn1(1, 1)
         v_quant_x(3)
+        v_ag1(1, 1)
+        s_sqrt(1)
         v_group_w2(0)
         v_eps(1)
-        g_widen_gb2()
-        v_group_w2(1)
-        v_recip(1)
         pe_mx1(2, 0)
         pe_mx1(2, 1)
+        v_recip(1)
         s_hevac(0, 0)
-        v_z1(1, 0)
         s_hevac(0, 1)
-        v_z1(1, 1)
+        v_negmean_r(1)
         s_hevac(0, 2)
+        s_z1(1, 0)
+        v_z1(1, 1)
         s_hevac(0, 3)
         v_bn1(2, 0)
         pe_zt(1, 0)
@@ -498,12 +511,15 @@ def tile_rlstmcell_pa_t_kernel(tc, c_att, w1, w2, g1, g2, b1, b2, out):
         v_ag1(2, 1)
         s_regroup(0)
         s_sqrt(2)
-        v_quant_w2()
+        v_group_w2(1)
         pe_mx1(3, 0)
         for t in range(2, NPAIR):
             v_quant_x(t + 2)
             pe_warm_y1(t + 1, 1)
             pe_mx1(t + 1, 1)
+            if t == 2:
+                nc.sync.dma_start(out=b2b[:], in_=b2.partition_broadcast(P))
+                g_widen_b2()
             v_ag2(t - 3, 1)
             v_eps(t)
             v_quant_h(t - 2)
@@ -512,6 +528,8 @@ def tile_rlstmcell_pa_t_kernel(tc, c_att, w1, w2, g1, g2, b1, b2, out):
             g_scale(t - 4, 0)
             if t < 4:
                 v_negmean_r(t)
+            if t == 2:
+                v_quant_w2()
             v_bn1(t + 1, 0)
             s_hevac(t - 1, 1)
             s_hevac(t - 1, 2)
@@ -536,7 +554,8 @@ def tile_rlstmcell_pa_t_kernel(tc, c_att, w1, w2, g1, g2, b1, b2, out):
             s_regroup(t - 1)
             v_bn2(t - 2, 1)
             s_sqrt(t + 1)
-            s_xevac(t + 4)
+            x_part(nc.vector.tensor_copy, t + 4, slice(112, P))
+            x_part(nc.scalar.copy, t + 4, slice(0, 112))
             v_ag2(t - 2, 0)
             load_x(t + 11)
             pe_mx1(t + 2, 0)
@@ -586,10 +605,12 @@ def tile_rlstmcell_pa_t_kernel(tc, c_att, w1, w2, g1, g2, b1, b2, out):
         v_bn2(31, 1)
         v_ag2(31, 0)
         v_finish(30, 0)
+        store_tile(30, 0)
         v_ag2(31, 1)
+        s_scale(30, 1)
+        g_bias_tile(30, 1)
+        store_tile(30, 1)
         s_sqrt(35)
-        v_finish(30, 1)
-        store(30)
         s_eps(35)
         v_gain2(31, 0)
         v_gain2(31, 1)

@@ -554,8 +554,7 @@ def tile_rlstmcell_pa_t_kernel(tc, c_att, w1, w2, g1, g2, b1, b2, out):
             s_regroup(t - 1)
             v_bn2(t - 2, 1)
             s_sqrt(t + 1)
-            x_part(nc.vector.tensor_copy, t + 4, slice(112, P))
-            x_part(nc.scalar.copy, t + 4, slice(0, 112))
+            s_xevac(t + 4)
             v_ag2(t - 2, 0)
             load_x(t + 11)
             pe_mx1(t + 2, 0)

@@ -401,23 +401,24 @@ def tile_rlstmcell_pa_t_kernel(tc, c_att, w1, w2, g1, g2, b1, b2, out):
                 op0=ALU.mult, op1=ALU.add,
             )
 
-        def g_scale(q, i):
+        def g_scale(q, i, cols=slice(0, D)):
             if not valid(q):
                 return
             rr = small_set(q + LAG2)[2]
             a = a_t[q]
             nc.gpsimd.tensor_scalar(
-                out=a[:, i, :], in0=a[:, i, :], scalar1=rr[:, 2 + i : 3 + i], scalar2=0.0,
+                out=a[:, i, cols], in0=a[:, i, cols], scalar1=rr[:, 2 + i : 3 + i], scalar2=0.0,
                 op0=ALU.mult, op1=ALU.add,
             )
 
-        def s_scale(q, i):
+        def s_scale(q, i, cols=slice(0, D)):
             if not valid(q):
                 return
             rr = small_set(q + LAG2)[2]
             a = a_t[q]
             nc.scalar.activation(
-                out=a[:, i, :], in_=a[:, i, :], func=ACT.Identity, scale=rr[:, 2 + i : 3 + i]
+                out=a[:, i, cols], in_=a[:, i, cols], func=ACT.Identity,
+                scale=rr[:, 2 + i : 3 + i],
             )
 
         def g_bias(q):
@@ -526,6 +527,7 @@ def tile_rlstmcell_pa_t_kernel(tc, c_att, w1, w2, g1, g2, b1, b2, out):
             v_recip(t)
             s_hevac(t - 1, 0)
             g_scale(t - 4, 0)
+            g_scale(t - 4, 1, slice(0, 128))
             if t < 4:
                 v_negmean_r(t)
             if t == 2:
@@ -560,7 +562,7 @@ def tile_rlstmcell_pa_t_kernel(tc, c_att, w1, w2, g1, g2, b1, b2, out):
             pe_mx1(t + 2, 0)
             pe_warm_y1(t + 2, 1)
             pe_zt(t, 1)
-            s_scale(t - 4, 1)
+            s_scale(t - 4, 1, slice(128, D))
 
         v_ag2(29, 1)
         v_quant_h(30)

@@ -521,13 +521,12 @@ def tile_rlstmcell_pa_t_kernel(tc, c_att, w1, w2, g1, g2, b1, b2, out):
             if t == 2:
                 nc.sync.dma_start(out=b2b[:], in_=b2.partition_broadcast(P))
                 g_widen_b2()
-            v_ag2(t - 3, 1)
             v_eps(t)
             v_quant_h(t - 2)
             v_recip(t)
+            v_ag2(t - 3, 1)
             s_hevac(t - 1, 0)
             g_scale(t - 4, 0)
-            g_scale(t - 4, 1, slice(0, 128))
             if t < 4:
                 v_negmean_r(t)
             if t == 2:
@@ -538,17 +537,18 @@ def tile_rlstmcell_pa_t_kernel(tc, c_att, w1, w2, g1, g2, b1, b2, out):
             if t >= 4:
                 v_negmean_r(t)
             v_gain2(t - 3, 0)
+            s_hevac(t - 1, 3)
             s_z1(t, 0)
             v_gain2(t - 3, 1)
             pe_mx2(t - 2, 0)
             pe_mx2(t - 2, 1)
             pe_xt(t + 4)
             pe_warm_y1(t + 2, 0)
-            s_hevac(t - 1, 3)
             v_bn1(t + 1, 1)
             s_z1(t, 1)
             g_bias(t - 5)
             store(t - 5)
+            g_scale(t - 4, 1, slice(0, 96))
             v_ag1(t + 1, 0)
             v_bn2(t - 2, 0)
             v_ag1(t + 1, 1)
@@ -562,7 +562,7 @@ def tile_rlstmcell_pa_t_kernel(tc, c_att, w1, w2, g1, g2, b1, b2, out):
             pe_mx1(t + 2, 0)
             pe_warm_y1(t + 2, 1)
             pe_zt(t, 1)
-            s_scale(t - 4, 1, slice(128, D))
+            s_scale(t - 4, 1, slice(96, D))
 
         v_ag2(29, 1)
         v_quant_h(30)

@@ -73,21 +73,29 @@ def tile_rlstmcell_pa_t_kernel(tc, c_att, w1, w2, g1, g2, b1, b2, out):
         ident = const.tile([P, P], F32, name="ident")
         make_identity(nc, ident[:])
 
-        w1raw = const.tile([P, 4, D], BF16, name="w1raw")
+        w1raw_a = const.tile([P, 4, 2 * P], BF16, name="w1raw_a")
+        w1raw_b = const.tile([P, 4, 2 * P], BF16, name="w1raw_b")
+        w1raw = [w1raw_a, w1raw_b]
         w2raw = const.tile([P, 4, D], BF16, name="w2raw")
         g2b = const.tile([P, D], BF16, name="g2b")
         b2b = const.tile([P, D], BF16, name="b2b")
-        nc.sync.dma_start(
-            out=w1raw[:].rearrange("p (u e) n -> p u (e n)", u=2),
-            in_=w1.rearrange("(u p e) n -> p u (e n)", u=2, e=2),
-        )
+        def load_w1(half):
+            cols = slice(half * 2 * P, (half + 1) * 2 * P)
+            for u in range(2):
+                nc.sync.dma_start(
+                    out=w1raw[half][:, 2 * u : 2 * u + 2, :],
+                    in_=w1[u * 2 * P : (u + 1) * 2 * P, cols].rearrange("(p e) n -> p e n", e=2),
+                )
+
+        load_w1(0)
         load_x(0)
+        load_w1(1)
+        load_x(1)
         nc.sync.dma_start(out=gbr[0:4, :], in_=g1.rearrange("(j p) -> j p", p=P))
         nc.sync.dma_start(out=gbr[4:8, :], in_=b1.rearrange("(j p) -> j p", p=P))
-        load_x(1)
-        nc.sync.dma_start(out=w2raw[:], in_=w2.rearrange("(t p) n -> p t n", p=P))
         load_x(2)
         load_x(3)
+        nc.sync.dma_start(out=w2raw[:], in_=w2.rearrange("(t p) n -> p t n", p=P))
         for q in range(4, FIRST_LOADS):
             load_x(q)
 
@@ -101,11 +109,17 @@ def tile_rlstmcell_pa_t_kernel(tc, c_att, w1, w2, g1, g2, b1, b2, out):
         gbf = const.tile([P, P], F32, name="gbf")
         gb1 = const.tile([P, 8], F32, name="gb1")
 
-        def v_prepare_w1():
-            nc.vector.tensor_copy(out=w1g[:], in_=w1raw[:].rearrange("p t n -> p n t"))
+        def v_group_w1(half):
+            cols = slice(half * 2 * P, (half + 1) * 2 * P)
+            nc.vector.tensor_copy(
+                out=w1g[:, cols, :], in_=w1raw[half][:].rearrange("p t n -> p n t")
+            )
+
+        def v_quant_w1(half):
+            cols = slice(half * 2 * P, (half + 1) * 2 * P)
             nc.vector.quantize_mx(
-                out=w1q[:].bitcast(FP8X4), scales=w1s[:],
-                in_=w1g[:].rearrange("p n t -> p (n t)"),
+                out=w1q[:, cols].bitcast(FP8X4), scales=w1s[:, cols],
+                in_=w1g[:, cols, :].rearrange("p n t -> p (n t)"),
             )
 
         def v_group_w2(half):
@@ -126,10 +140,13 @@ def tile_rlstmcell_pa_t_kernel(tc, c_att, w1, w2, g1, g2, b1, b2, out):
                 out=gbf[:], in0=gbr[:], scalar1=1.0, scalar2=0.0, op0=ALU.mult, op1=ALU.add
             )
 
+        gbt = ps_y2.tile([P, D], F32, name="gbt", tag="y2")
+
         def pe_turn_gb1():
-            gbt = ps_tp.tile([P, 2, PAIR], F32, name="gbt", tag="tp")
-            nc.tensor.transpose(gbt[:, 0, 0:P], gbf[:], ident[:])
-            nc.vector.tensor_copy(out=gb1[:], in_=gbt[:, 0, 0:8])
+            nc.tensor.transpose(gbt[:, 0:P], gbf[:], ident[:])
+
+        def v_keep_gb1():
+            nc.vector.tensor_copy(out=gb1[:], in_=gbt[:, 0:8])
 
         def g_widen_b2():
             for i in range(2):
@@ -443,7 +460,9 @@ def tile_rlstmcell_pa_t_kernel(tc, c_att, w1, w2, g1, g2, b1, b2, out):
                 return
             nc.sync.dma_start(out=o_pairs[q], in_=a_t[q][:].rearrange("p i d -> p (i d)"))
 
-        v_prepare_w1()
+        v_group_w1(0)
+        v_group_w1(1)
+        v_quant_w1(0)
         g_widen_gb1()
         for q in range(FIRST_LOADS, 9):
             load_x(q)
@@ -453,56 +472,57 @@ def tile_rlstmcell_pa_t_kernel(tc, c_att, w1, w2, g1, g2, b1, b2, out):
         pe_warm_y1(0, 0, 4)
         pe_xt(0)
         pe_xt(1)
-        pe_warm_y1(0, 1, 2)
+        pe_xt(2, ps_y2, "y2")
         s_xevac(0)
         s_xevac(1)
         v_quant_x(0)
+        v_quant_w1(1)
         v_quant_x(1)
         pe_mx1(0, 0)
         pe_mx1(0, 1)
-        pe_xt(2)
+        s_xevac(2)
+        pe_xt(3)
         pe_mx1(1, 0)
         pe_mx1(1, 1)
-        s_xevac(2)
+        pe_turn_gb1()
+        s_xevac(3)
         v_bn1(0, 0)
         v_bn1(0, 1)
         v_ag1(0, 0)
         v_ag1(0, 1)
-        pe_turn_gb1()
-        pe_xt(3)
-        pe_xt(4, ps_y2, "y2")
-        pe_xt(5, ps_y2, "y2")
-        new_zt(0, 0)
-        pe_warm(zt_t[(0, 0)][:].rearrange("p j w -> p (j w)"), 4)
+        pe_xt(4)
         s_sqrt(0)
-        s_xevac(3)
         s_xevac(4)
         v_bn1(1, 0)
-        v_eps(0)
         v_quant_x(2)
+        v_eps(0)
+        v_bn1(1, 1)
         v_recip(0)
         v_ag1(1, 0)
+        v_ag1(1, 1)
+        s_sqrt(1)
+        new_zt(0, 0)
+        pe_warm(zt_t[(0, 0)][:].rearrange("p j w -> p (j w)"), 4)
         v_negmean_r(0)
         s_z1(0, 0)
         v_z1(0, 1)
+        v_keep_gb1()
+        pe_xt(5, ps_y2, "y2")
+        v_eps(1)
+        v_quant_x(3)
+        v_recip(1)
         s_xevac(5)
         pe_zt(0, 0)
         pe_zt(0, 1)
-        v_bn1(1, 1)
-        v_quant_x(3)
-        v_ag1(1, 1)
-        s_sqrt(1)
-        v_group_w2(0)
-        v_eps(1)
         pe_mx1(2, 0)
         pe_mx1(2, 1)
-        v_recip(1)
+        v_group_w2(0)
+
+        v_z1(1, 0)
+        v_z1(1, 1)
         s_hevac(0, 0)
         s_hevac(0, 1)
-        v_negmean_r(1)
         s_hevac(0, 2)
-        s_z1(1, 0)
-        v_z1(1, 1)
         s_hevac(0, 3)
         v_bn1(2, 0)
         pe_zt(1, 0)

@@ -73,23 +73,15 @@ def tile_rlstmcell_pa_t_kernel(tc, c_att, w1, w2, g1, g2, b1, b2, out):
         ident = const.tile([P, P], F32, name="ident")
         make_identity(nc, ident[:])
 
-        w1raw_a = const.tile([P, 4, 2 * P], BF16, name="w1raw_a")
-        w1raw_b = const.tile([P, 4, 2 * P], BF16, name="w1raw_b")
-        w1raw = [w1raw_a, w1raw_b]
+        w1raw = const.tile([P, 4, D], BF16, name="w1raw")
         w2raw = const.tile([P, 4, D], BF16, name="w2raw")
         g2b = const.tile([P, D], BF16, name="g2b")
         b2b = const.tile([P, D], BF16, name="b2b")
-        def load_w1(half):
-            cols = slice(half * 2 * P, (half + 1) * 2 * P)
-            for u in range(2):
-                nc.sync.dma_start(
-                    out=w1raw[half][:, 2 * u : 2 * u + 2, :],
-                    in_=w1[u * 2 * P : (u + 1) * 2 * P, cols].rearrange("(p e) n -> p e n", e=2),
-                )
-
-        load_w1(0)
+        nc.sync.dma_start(
+            out=w1raw[:].rearrange("p (u e) n -> p u (e n)", u=2),
+            in_=w1.rearrange("(u p e) n -> p u (e n)", u=2, e=2),
+        )
         load_x(0)
-        load_w1(1)
         load_x(1)
         nc.sync.dma_start(out=gbr[0:4, :], in_=g1.rearrange("(j p) -> j p", p=P))
         nc.sync.dma_start(out=gbr[4:8, :], in_=b1.rearrange("(j p) -> j p", p=P))
@@ -112,7 +104,7 @@ def tile_rlstmcell_pa_t_kernel(tc, c_att, w1, w2, g1, g2, b1, b2, out):
         def v_group_w1(half):
             cols = slice(half * 2 * P, (half + 1) * 2 * P)
             nc.vector.tensor_copy(
-                out=w1g[:, cols, :], in_=w1raw[half][:].rearrange("p t n -> p n t")
+                out=w1g[:, cols, :], in_=w1raw[:, :, cols].rearrange("p t n -> p n t")
             )
 
         def v_quant_w1(half):
@@ -475,8 +467,8 @@ def tile_rlstmcell_pa_t_kernel(tc, c_att, w1, w2, g1, g2, b1, b2, out):
         pe_xt(2, ps_y2, "y2")
         s_xevac(0)
         s_xevac(1)
-        v_quant_x(0)
         v_quant_w1(1)
+        v_quant_x(0)
         v_quant_x(1)
         pe_mx1(0, 0)
         pe_mx1(0, 1)

@@ -97,7 +97,6 @@ def tile_rlstmcell_pa_t_kernel(tc, c_att, w1, w2, g1, g2, b1, b2, out):
         w2g = const.tile([P, D, 4], BF16, name="w2g", align_bytes=64)
         w2q = const.tile([P, D], U32, name="w2q", align_bytes=64)
         w2s = const.tile([P, D], U8, name="w2s", align_bytes=64)
-        b2f = const.tile([P, 2, D], F32, name="b2f")
         gbf = const.tile([P, P], F32, name="gbf")
         gb1 = const.tile([P, 8], F32, name="gb1")
 
@@ -139,12 +138,6 @@ def tile_rlstmcell_pa_t_kernel(tc, c_att, w1, w2, g1, g2, b1, b2, out):
 
         def v_keep_gb1():
             nc.vector.tensor_copy(out=gb1[:], in_=gbt[:, 0:8])
-
-        def g_widen_b2():
-            for i in range(2):
-                nc.gpsimd.tensor_scalar(
-                    out=b2f[:, i, :], in0=b2b[:], scalar1=1.0, scalar2=0.0, op0=ALU.mult, op1=ALU.add
-                )
 
         def pe_warm(bank, times=1):
             for k in range(times):
@@ -406,7 +399,7 @@ def tile_rlstmcell_pa_t_kernel(tc, c_att, w1, w2, g1, g2, b1, b2, out):
             rr = small_set(q + LAG2)[2]
             a = a_t[q]
             nc.vector.scalar_tensor_tensor(
-                out=a[:, i, :], in0=a[:, i, :], scalar=rr[:, 2 + i : 3 + i], in1=b2f[:, i, :],
+                out=a[:, i, :], in0=a[:, i, :], scalar=rr[:, 2 + i : 3 + i], in1=b2b[:],
                 op0=ALU.mult, op1=ALU.add,
             )
 
@@ -434,12 +427,14 @@ def tile_rlstmcell_pa_t_kernel(tc, c_att, w1, w2, g1, g2, b1, b2, out):
             if not valid(q):
                 return
             a = a_t[q]
-            nc.gpsimd.tensor_tensor(out=a[:], in0=a[:], in1=b2f[:], op=ALU.add)
+            nc.gpsimd.tensor_tensor(
+                out=a[:], in0=a[:], in1=b2b[:].unsqueeze(1).to_broadcast([P, 2, D]), op=ALU.add
+            )
 
         def g_bias_tile(q, i):
             a = a_t[q]
             nc.gpsimd.tensor_tensor(
-                out=a[:, i, :], in0=a[:, i, :], in1=b2f[:, i, :], op=ALU.add
+                out=a[:, i, :], in0=a[:, i, :], in1=b2b[:], op=ALU.add
             )
 
         def store_tile(q, i):
@@ -532,7 +527,6 @@ def tile_rlstmcell_pa_t_kernel(tc, c_att, w1, w2, g1, g2, b1, b2, out):
             pe_mx1(t + 1, 1)
             if t == 2:
                 nc.sync.dma_start(out=b2b[:], in_=b2.partition_broadcast(P))
-                g_widen_b2()
             v_eps(t)
             v_quant_h(t - 2)
             v_recip(t)

@@ -460,6 +460,7 @@ def tile_rlstmcell_pa_t_kernel(tc, c_att, w1, w2, g1, g2, b1, b2, out):
         pe_xt(0)
         pe_xt(1)
         pe_xt(2, ps_y2, "y2")
+        pe_warm_y1(0, 1, 3)
         s_xevac(0)
         s_xevac(1)
         v_quant_w1(1)

from contextlib import ExitStack

import concourse.mybir as mybir
from concourse.masks import make_identity

F32 = mybir.dt.float32
BF16 = mybir.dt.bfloat16
U32 = mybir.dt.uint32
U8 = mybir.dt.uint8
FP8X4 = mybir.dt.float8_e4m3fn_x4
ACT = mybir.ActivationFunctionType
ALU = mybir.AluOpType

P = 128
D = 512
TOKENS = 512 * 16
PAIR = 2 * P
NPAIR = TOKENS // PAIR
EPS = 1e-9
FLOPS = 2 * 2 * TOKENS * D * D
LAG2 = 4
FIRST_LOADS = 7


def tile_rlstmcell_pa_t_kernel(tc, c_att, w1, w2, g1, g2, b1, b2, out):
    nc = tc.nc
    x_pairs = c_att.flatten_outer_dims().rearrange("(q p i) d -> q p (i d)", p=P, i=2)
    o_pairs = out.flatten_outer_dims().rearrange("(q p i) d -> q p (i d)", p=P, i=2)

    with ExitStack() as ctx:
        ctx.enter_context(tc.manual_schedule())
        const = ctx.enter_context(tc.tile_pool(name="const", bufs=1))
        xin = ctx.enter_context(tc.tile_pool(name="xin", bufs=FIRST_LOADS + 6))
        work3 = ctx.enter_context(tc.tile_pool(name="work3", bufs=4))
        work6 = ctx.enter_context(tc.tile_pool(name="work6", bufs=6))
        ps_tp = ctx.enter_context(tc.psum_pool(name="ps_tp", bufs=2))
        ps_y1 = ctx.enter_context(tc.psum_pool(name="ps_y1", bufs=4))
        ps_y2 = ctx.enter_context(tc.psum_pool(name="ps_y2", bufs=2))

        x_t = {}
        xt_t = {}
        xg_t = {}
        xq_t = {}
        y1_t = {}
        z_t = {}
        zt_t = {}
        ht_t = {}
        hg_t = {}
        hq_t = {}
        y2_t = {}
        a_t = {}
        st1_t = {}
        st2_t = {}
        set_t = {}

        def valid(q):
            return 0 <= q < NPAIR

        def load_x(q):
            if not valid(q):
                return
            x_sb = xin.tile([P, 2 * D], BF16, name="x_sb")
            nc.sync.dma_start(out=x_sb[:], in_=x_pairs[q])
            x_t[q] = x_sb

        one = const.tile([P, 1], F32, name="one")
        nc.vector.memset(one[:], 1.0)
        nc.scalar.activation(out=one[:], in_=one[:], func=ACT.Sqrt)
        eps = const.tile([P, 1], F32, name="eps")
        nc.vector.memset(eps[:], EPS)
        gbr = const.tile([P, P], BF16, name="gbr")
        nc.vector.memset(gbr[:], 0.0)
        ident = const.tile([P, P], F32, name="ident")
        make_identity(nc, ident[:])

        w1raw = const.tile([P, 4, D], BF16, name="w1raw")
        w2raw = const.tile([P, 4, D], BF16, name="w2raw")
        g2b = const.tile([P, D], BF16, name="g2b")
        b2b = const.tile([P, D], BF16, name="b2b")
        nc.sync.dma_start(
            out=w1raw[:].rearrange("p (u e) n -> p u (e n)", u=2),
            in_=w1.rearrange("(u p e) n -> p u (e n)", u=2, e=2),
        )
        load_x(0)
        load_x(1)
        nc.sync.dma_start(out=gbr[0:4, :], in_=g1.rearrange("(j p) -> j p", p=P))
        nc.sync.dma_start(out=gbr[4:8, :], in_=b1.rearrange("(j p) -> j p", p=P))
        load_x(2)
        load_x(3)
        nc.sync.dma_start(out=w2raw[:], in_=w2.rearrange("(t p) n -> p t n", p=P))
        for q in range(4, FIRST_LOADS):
            load_x(q)

        w1g = const.tile([P, D, 4], BF16, name="w1g", align_bytes=64)
        w1q = const.tile([P, D], U32, name="w1q", align_bytes=64)
        w1s = const.tile([P, D], U8, name="w1s", align_bytes=64)
        w2g = const.tile([P, D, 4], BF16, name="w2g", align_bytes=64)
        w2q = const.tile([P, D], U32, name="w2q", align_bytes=64)
        w2s = const.tile([P, D], U8, name="w2s", align_bytes=64)
        gbf = const.tile([P, P], F32, name="gbf")
        gb1 = const.tile([P, 8], F32, name="gb1")

        def v_group_w1(half):
            cols = slice(half * 2 * P, (half + 1) * 2 * P)
            nc.vector.tensor_copy(
                out=w1g[:, cols, :], in_=w1raw[:, :, cols].rearrange("p t n -> p n t")
            )

        def v_quant_w1(half):
            cols = slice(half * 2 * P, (half + 1) * 2 * P)
            nc.vector.quantize_mx(
                out=w1q[:, cols].bitcast(FP8X4), scales=w1s[:, cols],
                in_=w1g[:, cols, :].rearrange("p n t -> p (n t)"),
            )

        def v_group_w2(half):
            w = slice(half * 2 * P, (half + 1) * 2 * P)
            nc.vector.tensor_copy(
                out=w2g[:, w, :].rearrange("p (c i) j -> p c j i", i=4),
                in_=w2raw[:, :, w].rearrange("p j (c i) -> p c j i", i=4),
            )

        def v_quant_w2():
            nc.vector.quantize_mx(
                out=w2q[:].bitcast(FP8X4), scales=w2s[:],
                in_=w2g[:].rearrange("p n t -> p (n t)"),
            )

        def g_widen_gb1():
            nc.gpsimd.tensor_scalar(
                out=gbf[:], in0=gbr[:], scalar1=1.0, scalar2=0.0, op0=ALU.mult, op1=ALU.add
            )

        gbt = ps_y2.tile([P, D], F32, name="gbt", tag="y2")

        def pe_turn_gb1():
            nc.tensor.transpose(gbt[:, 0:P], gbf[:], ident[:])

        def v_keep_gb1():
            nc.vector.tensor_copy(out=gb1[:], in_=gbt[:, 0:8])

        def pe_warm(bank, times=1):
            for k in range(times):
                nc.tensor.matmul(
                    out=bank[:, (k % 4) * P : (k % 4 + 1) * P],
                    lhsT=ident[:], rhs=ident[:], start=True, stop=True,
                )

        def pe_xt(q, pool=ps_tp, tag="tp"):
            if not valid(q):
                return
            xt = pool.tile([P, 2, 2, P], F32, name="xt", tag=tag)
            x32 = x_t[q][:].bitcast(F32)
            for i in range(2):
                for u in range(2):
                    c0 = 256 * i + 128 * u
                    nc.tensor.transpose(xt[:, i, u, :], x32[:, c0 : c0 + P], ident[:])
            xt_t[q] = xt

        def v_xevac(q):
            xg = work3.tile([P, 4 * PAIR], BF16, name="xg", align_bytes=64)
            nc.vector.tensor_copy(
                out=xg[:].bitcast(F32).rearrange("p (i w u) -> p i w u", i=2, u=2),
                in_=xt_t[q][:].rearrange("p i u w -> p i w u"),
            )
            xg_t[q] = xg

        def x_part(copy, q, cols):
            if not valid(q):
                return
            if q not in xg_t:
                xg = work3.tile([P, 4 * PAIR], BF16, name="xg", align_bytes=64)
                xg_t[q] = xg
            xg32 = xg_t[q][:].bitcast(F32).rearrange("p (i w u) -> p i w u", i=2, u=2)
            xt = xt_t[q][:].rearrange("p i u w -> p i w u")
            copy(out=xg32[:, :, cols, :], in_=xt[:, :, cols, :])

        def s_xevac(q):
            if not valid(q):
                return
            xg = work3.tile([P, 4 * PAIR], BF16, name="xg", align_bytes=64)
            nc.scalar.copy(
                out=xg[:].bitcast(F32).rearrange("p (i w u) -> p i w u", i=2, u=2),
                in_=xt_t[q][:].rearrange("p i u w -> p i w u"),
            )
            xg_t[q] = xg

        def v_quant_x(q):
            if not valid(q):
                return
            xq = work3.tile([P, PAIR], U32, name="xq", align_bytes=64)
            xs = work3.tile([P, PAIR], U8, name="xs", align_bytes=64)
            nc.vector.quantize_mx(out=xq[:].bitcast(FP8X4), scales=xs[:], in_=xg_t[q][:])
            xq_t[q] = (xq, xs)

        def pe_mx(q, i, src, wq, ws, pool, nm, dst):
            if not valid(q):
                return
            codes, scales = src[q]
            acc = dst[(q, i)] if (q, i) in dst else pool.tile([P, D], F32, name=nm)
            cols = slice(i * P, (i + 1) * P)
            nc.tensor.matmul_mx(
                out=acc[:],
                lhsT=codes[:, cols].bitcast(FP8X4),
                lhsT_scale=scales[:, cols],
                rhs=wq[:].bitcast(FP8X4),
                rhs_scale=ws[:],
                start=True,
                stop=True,
            )
            dst[(q, i)] = acc

        def pe_warm_y(dst, q, i, times=1):
            if (q, i) not in dst:
                acc = ps_y1.tile([P, D], F32, name="y1")
                dst[(q, i)] = acc
            pe_warm(dst[(q, i)], times)

        def pe_warm_y1(q, i, times=1):
            pe_warm_y(y1_t, q, i, times)

        def pe_mx1(q, i):
            pe_mx(q, i, xq_t, w1q, w1s, ps_y1, "y1", y1_t)

        def pe_mx2(q, i):
            pe_mx(q, i, hq_t, w2q, w2s, ps_y2, "y2", y2_t)

        def pe_mx2_last(q, i):
            pe_mx(q, i, hq_t, w2q, w2s, ps_y1, "y1", y2_t)

        def span(s):
            lo = 0 if valid(s) else 2
            hi = 4 if valid(s - LAG2) else 2
            return lo, hi

        def small_set(s):
            if s not in set_t:
                mvr = work6.tile([P, 4, 3], F32, name="mvr")
                sd = work6.tile([P, 4], F32, name="sd")
                set_t[s] = (mvr, sd, mvr[:, :, 2])
            return set_t[s]

        def v_bn1(q, i):
            if not valid(q):
                return
            if i == 0:
                st1 = work3.tile([P, 2, 6], F32, name="st1")
                st1_t[q] = st1
            nc.vector.bn_stats(out=st1_t[q][:, i, :], in_=y1_t[(q, i)][:])

        def v_ag1(q, i):
            if not valid(q):
                return
            nc.vector.bn_aggr(out=small_set(q)[0][:, i, 0:2], in_=st1_t[q][:, i, :])

        def v_bn2(q, i):
            if not valid(q):
                return
            if i == 0:
                st2 = work3.tile([P, 2, 6], F32, name="st2")
                st2_t[q] = st2
            nc.vector.bn_stats(out=st2_t[q][:, i, :], in_=y2_t[(q, i)][:])

        def v_ag2(q, i):
            if not valid(q):
                return
            nc.vector.bn_aggr(out=small_set(q + LAG2)[0][:, 2 + i, 0:2], in_=st2_t[q][:, i, :])

        def s_sqrt(s):
            lo, hi = span(s)
            if lo >= hi:
                return
            mv, sd, rr = small_set(s)
            nc.scalar.activation(out=sd[:, lo:hi], in_=mv[:, lo:hi, 1], func=ACT.Sqrt)

        nmr_t = {}

        def v_eps(s):
            lo, hi = span(s)
            if lo >= hi:
                return
            sd = small_set(s)[1]
            nc.vector.tensor_scalar_add(out=sd[:, lo:hi], in0=sd[:, lo:hi], scalar1=EPS)

        def s_eps(s):
            lo, hi = span(s)
            sd = small_set(s)[1]
            nc.scalar.activation(
                out=sd[:, lo:hi], in_=sd[:, lo:hi], func=ACT.Identity, bias=eps[:, 0:1]
            )

        def v_recip(s):
            lo, hi = span(s)
            if lo >= hi:
                return
            mv, sd, rr = small_set(s)
            nc.vector.reciprocal(out=rr[:, lo:hi], in_=sd[:, lo:hi])

        def v_negmean_r(q):
            if not valid(q):
                return
            mvr = small_set(q)[0]
            nmr = work3.tile([P, 2], F32, name="nmr")
            nc.vector.tensor_reduce(
                out=nmr[:], in_=mvr[:, 0:2, 0:3:2], axis=mybir.AxisListType.X, op=ALU.mult,
                negate=True,
            )
            nmr_t[q] = nmr

        def s_z1(q, i):
            if not valid(q):
                return
            rr = small_set(q)[2]
            if q not in z_t:
                z_new = work3.tile([P, 2, D], F32, name="z")
                z_t[q] = z_new
            nc.scalar.activation(
                out=z_t[q][:, i, :], in_=y1_t[(q, i)][:], func=ACT.Identity,
                scale=rr[:, i : i + 1], bias=nmr_t[q][:, i : i + 1],
            )

        def v_z1(q, i):
            mvr = small_set(q)[0]
            if q not in z_t:
                z_new = work3.tile([P, 2, D], F32, name="z")
                z_t[q] = z_new
            nc.vector.tensor_scalar(
                out=z_t[q][:, i, :], in0=y1_t[(q, i)][:],
                scalar1=mvr[:, i, 0:1], scalar2=mvr[:, i, 2:3],
                op0=ALU.subtract, op1=ALU.mult,
            )

        def new_zt(q, h):
            zt = ps_tp.tile([P, 2, PAIR], F32, name="zt", tag="tp")
            zt_t[(q, h)] = zt

        def pe_zt(q, h):
            if not valid(q):
                return
            z = z_t[q]
            if (q, h) not in zt_t:
                new_zt(q, h)
            zt = zt_t[(q, h)]
            for jj in range(2):
                j = 2 * h + jj
                for i in range(2):
                    nc.tensor.transpose(
                        zt[:, jj, i * P : (i + 1) * P], z[:, i, j * P : (j + 1) * P], ident[:]
                    )

        def s_hevac(q, j):
            if not valid(q):
                return
            if q not in ht_t:
                ht_new = work3.tile([P, 4, PAIR], BF16, name="ht")
                ht_t[q] = ht_new
            nc.scalar.activation(
                out=ht_t[q][:, j, :], in_=zt_t[(q, j // 2)][:, j % 2, :], func=ACT.Relu,
                scale=gb1[:, j : j + 1], bias=gb1[:, 4 + j : 5 + j],
            )

        def s_regroup(q):
            if not valid(q):
                return
            if q not in hg_t:
                hg_new = work3.tile([P, PAIR, 4], BF16, name="hg", align_bytes=64)
                hg_t[q] = hg_new
            nc.scalar.copy(
                out=hg_t[q][:].rearrange("p (c i) j -> p c j i", i=4),
                in_=ht_t[q][:].rearrange("p j (c i) -> p c j i", i=4),
            )

        def v_quant_h(q):
            if not valid(q):
                return
            hq = work3.tile([P, PAIR], U32, name="hq", align_bytes=64)
            hs = work3.tile([P, PAIR], U8, name="hs", align_bytes=64)
            nc.vector.quantize_mx(
                out=hq[:].bitcast(FP8X4), scales=hs[:],
                in_=hg_t[q][:].rearrange("p w j -> p (w j)"),
            )
            hq_t[q] = (hq, hs)

        def v_gain2(q, i):
            if not valid(q):
                return
            if q not in a_t:
                a_new = work6.tile([P, 2, D], F32, name="a")
                a_t[q] = a_new
            mv = small_set(q + LAG2)[0]
            nc.vector.scalar_tensor_tensor(
                out=a_t[q][:, i, :], in0=y2_t[(q, i)][:], scalar=mv[:, 2 + i, 0:1], in1=g2b[:],
                op0=ALU.subtract, op1=ALU.mult,
            )

        def v_finish(q, i):
            if not valid(q):
                return
            rr = small_set(q + LAG2)[2]
            a = a_t[q]
            nc.vector.scalar_tensor_tensor(
                out=a[:, i, :], in0=a[:, i, :], scalar=rr[:, 2 + i : 3 + i], in1=b2b[:],
                op0=ALU.mult, op1=ALU.add,
            )

        def g_scale(q, i, cols=slice(0, D)):
            if not valid(q):
                return
            rr = small_set(q + LAG2)[2]
            a = a_t[q]
            nc.gpsimd.tensor_scalar(
                out=a[:, i, cols], in0=a[:, i, cols], scalar1=rr[:, 2 + i : 3 + i], scalar2=0.0,
                op0=ALU.mult, op1=ALU.add,
            )

        def s_scale(q, i, cols=slice(0, D)):
            if not valid(q):
                return
            rr = small_set(q + LAG2)[2]
            a = a_t[q]
            nc.scalar.activation(
                out=a[:, i, cols], in_=a[:, i, cols], func=ACT.Identity,
                scale=rr[:, 2 + i : 3 + i],
            )

        def g_bias(q):
            if not valid(q):
                return
            a = a_t[q]
            nc.gpsimd.tensor_tensor(
                out=a[:], in0=a[:], in1=b2b[:].unsqueeze(1).to_broadcast([P, 2, D]), op=ALU.add
            )

        def g_bias_tile(q, i):
            a = a_t[q]
            nc.gpsimd.tensor_tensor(
                out=a[:, i, :], in0=a[:, i, :], in1=b2b[:], op=ALU.add
            )

        def store_tile(q, i):
            nc.sync.dma_start(
                out=o_pairs[q][:, i * D : (i + 1) * D], in_=a_t[q][:, i, :]
            )

        def store(q):
            if not valid(q):
                return
            nc.sync.dma_start(out=o_pairs[q], in_=a_t[q][:].rearrange("p i d -> p (i d)"))

        v_group_w1(0)
        v_group_w1(1)
        v_quant_w1(0)
        g_widen_gb1()
        for q in range(FIRST_LOADS, 9):
            load_x(q)
        nc.sync.dma_start(out=g2b[:], in_=g2.partition_broadcast(P))
        for q in range(9, 13):
            load_x(q)
        pe_warm_y1(0, 0, 4)
        pe_xt(0)
        pe_xt(1)
        pe_xt(2, ps_y2, "y2")
        pe_warm_y1(0, 1, 3)
        s_xevac(0)
        s_xevac(1)
        v_quant_w1(1)
        v_quant_x(0)
        v_quant_x(1)
        pe_mx1(0, 0)
        pe_mx1(0, 1)
        s_xevac(2)
        pe_xt(3)
        pe_mx1(1, 0)
        pe_mx1(1, 1)
        pe_turn_gb1()
        s_xevac(3)
        v_bn1(0, 0)
        v_bn1(0, 1)
        v_ag1(0, 0)
        v_ag1(0, 1)
        pe_xt(4)
        s_sqrt(0)
        s_xevac(4)
        v_bn1(1, 0)
        v_quant_x(2)
        v_eps(0)
        v_bn1(1, 1)
        v_recip(0)
        v_ag1(1, 0)
        v_ag1(1, 1)
        s_sqrt(1)
        new_zt(0, 0)
        pe_warm(zt_t[(0, 0)][:].rearrange("p j w -> p (j w)"), 4)
        v_negmean_r(0)
        s_z1(0, 0)
        v_z1(0, 1)
        v_keep_gb1()
        pe_xt(5, ps_y2, "y2")
        v_eps(1)
        v_quant_x(3)
        v_recip(1)
        s_xevac(5)
        pe_zt(0, 0)
        pe_zt(0, 1)
        pe_mx1(2, 0)
        pe_mx1(2, 1)
        v_group_w2(0)

        v_z1(1, 0)
        v_z1(1, 1)
        s_hevac(0, 0)
        s_hevac(0, 1)
        s_hevac(0, 2)
        s_hevac(0, 3)
        v_bn1(2, 0)
        pe_zt(1, 0)
        pe_zt(1, 1)
        v_bn1(2, 1)
        v_ag1(2, 0)
        v_ag1(2, 1)
        s_regroup(0)
        s_sqrt(2)
        v_group_w2(1)
        pe_mx1(3, 0)
        for t in range(2, NPAIR):
            v_quant_x(t + 2)
            pe_warm_y1(t + 1, 1)
            pe_mx1(t + 1, 1)
            if t == 2:
                nc.sync.dma_start(out=b2b[:], in_=b2.partition_broadcast(P))
            v_eps(t)
            v_quant_h(t - 2)
            v_recip(t)
            v_ag2(t - 3, 1)
            s_hevac(t - 1, 0)
            g_scale(t - 4, 0)
            if t < 4:
                v_negmean_r(t)
            if t == 2:
                v_quant_w2()
            v_bn1(t + 1, 0)
            s_hevac(t - 1, 1)
            s_hevac(t - 1, 2)
            if t >= 4:
                v_negmean_r(t)
            v_gain2(t - 3, 0)
            s_hevac(t - 1, 3)
            s_z1(t, 0)
            v_gain2(t - 3, 1)
            pe_mx2(t - 2, 0)
            pe_mx2(t - 2, 1)
            pe_xt(t + 4)
            pe_warm_y1(t + 2, 0)
            v_bn1(t + 1, 1)
            s_z1(t, 1)
            g_bias(t - 5)
            store(t - 5)
            g_scale(t - 4, 1, slice(0, 96))
            v_ag1(t + 1, 0)
            v_bn2(t - 2, 0)
            v_ag1(t + 1, 1)
            pe_zt(t, 0)
            s_regroup(t - 1)
            v_bn2(t - 2, 1)
            s_sqrt(t + 1)
            s_xevac(t + 4)
            v_ag2(t - 2, 0)
            load_x(t + 11)
            pe_mx1(t + 2, 0)
            pe_warm_y1(t + 2, 1)
            pe_zt(t, 1)
            s_scale(t - 4, 1, slice(96, D))

        v_ag2(29, 1)
        v_quant_h(30)
        v_eps(32)
        s_hevac(31, 0)
        s_sqrt(33)
        s_hevac(31, 1)
        s_hevac(31, 2)
        s_eps(33)
        s_hevac(31, 3)
        v_gain2(29, 0)
        v_recip(32)
        pe_mx2_last(30, 0)
        pe_mx2_last(30, 1)
        pe_warm_y(y2_t, 31, 0, 4)
        g_bias(27)
        store(27)
        v_gain2(29, 1)
        s_scale(28, 0)
        s_regroup(31)
        v_bn2(30, 0)
        v_recip(33)
        v_bn2(30, 1)
        s_scale(28, 1)
        v_ag2(30, 0)
        v_ag2(30, 1)
        v_finish(29, 0)
        v_quant_h(31)
        s_sqrt(34)
        pe_mx2_last(31, 0)
        pe_mx2_last(31, 1)
        v_finish(29, 1)
        s_eps(34)
        store(29)
        g_bias(28)
        store(28)
        v_gain2(30, 0)
        v_gain2(30, 1)
        v_bn2(31, 0)
        v_recip(34)
        v_bn2(31, 1)
        v_ag2(31, 0)
        v_finish(30, 0)
        store_tile(30, 0)
        v_ag2(31, 1)
        s_scale(30, 1)
        g_bias_tile(30, 1)
        store_tile(30, 1)
        s_sqrt(35)
        s_eps(35)
        v_gain2(31, 0)
        v_gain2(31, 1)
        v_recip(35)
        v_finish(31, 0)
        store_tile(31, 0)
        v_finish(31, 1)
        store_tile(31, 1)
